import numpy as np
import ml_dtypes


def mxq(x, axis, fmt="e4m3"):
    dtype, down = {"e4m3": (ml_dtypes.float8_e4m3fn, 7), "e5m2": (ml_dtypes.float8_e5m2, 14)}[fmt]
    v = np.moveaxis(np.asarray(x, np.float32).astype(ml_dtypes.bfloat16).astype(np.float64), axis, -1)
    blocks = v.reshape(v.shape[:-1] + (-1, 32))
    amax = np.abs(blocks).max(-1, keepdims=True)
    byte = np.maximum(np.where(amax > 0, np.frexp(amax)[1] - 1 + 127, 0) - down, 1)
    scale = np.exp2(byte - 127.0)
    codes = (blocks / scale).astype(np.float32).astype(dtype).astype(np.float64)
    return np.moveaxis((codes * scale).reshape(v.shape), -1, axis)


WIDE = False


def mx_kscale(k):
    if not WIDE:
        return np.ones(k)
    levels = np.array([10, -10, 5, -5, 0])
    a = np.random.permutation(np.resize(levels, k // 512 * 4)).reshape(k // 512, 4)
    idx = np.arange(k)
    return np.exp2(a[idx // 512, idx % 128 // 32])


BF16 = ml_dtypes.bfloat16


def bf(x):
    return np.asarray(x, np.float32).astype(BF16)


def f64(x):
    return np.asarray(x).astype(np.float64)


B, G, C, F, NC = 32, 14, 1024, 128, 4096
HW = G * G
KS = 3
P_GEM = 3.0
EPS_GEM = 1e-6
EPS_NORM = 1e-12


def l2n(v, axis):
    n = np.sqrt(np.sum(v * v, axis=axis, keepdims=True))
    return v / np.maximum(n, EPS_NORM)


def erf(v):
    a = np.clip(v, -7.0, 7.0)
    a2 = 2.0 * a * a
    term = a.copy()
    tot = a.copy()
    for n in range(1, 140):
        term = term * a2 / (2 * n + 1)
        tot = tot + term
    return 2.0 / np.sqrt(np.pi) * np.exp(-a * a) * tot


def gelu_erf(v):
    return 0.5 * v * (1.0 + erf(v / np.sqrt(2.0)))


def setup_inputs():
    s = mx_kscale(C)
    t = s / s.min()
    g = 2.0 ** np.round(0.5 * np.log2(np.mean(t * t)))
    return {"patch_tokens": bf(np.random.standard_normal((B, HW, C)) * 2.0 / G * t),
            "fc1_w": bf(np.random.standard_normal((C, F)) * (g / t)[:, None]),
            "fc1_b": bf(np.random.standard_normal(F) * 0.3)}


def reference(patch_tokens, fc1_w, fc1_b):
    x = f64(patch_tokens)
    padded = np.pad(x.reshape(B, G, G, C), ((0, 0), (KS - 1, 0), (KS // 2, KS // 2), (0, 0)))
    acc = np.zeros_like(x)
    for ki in range(KS):
        for kj in range(KS):
            y = padded[:, ki:ki + G, kj:kj + G, :].reshape(B, HW, C)
            acc = acc + np.maximum(l2n(x * y, 1), EPS_GEM) ** P_GEM
    pooled = (acc / (KS * KS)) ** (1.0 / P_GEM)
    tokens = l2n(pooled + x, 2)
    return gelu_erf((mxq(tokens, 2, "e4m3") @ mxq(f64(fc1_w), 0, "e4m3")) + f64(fc1_b))

@@ -1,0 +1,444 @@
+from contextlib import ExitStack
+
+import concourse.mybir as mybir
+from concourse.masks import make_identity
+
+F32 = mybir.dt.float32
+BF16 = mybir.dt.bfloat16
+U32 = mybir.dt.uint32
+U8 = mybir.dt.uint8
+FP8X4 = mybir.dt.float8_e4m3fn_x4
+ACT = mybir.ActivationFunctionType
+ALU = mybir.AluOpType
+
+P = 128
+IMAGES = 32
+GRID = 14
+TOKENS = GRID * GRID
+CHANNELS = 1024
+FEATURES = 128
+BLOCKS = CHANNELS // P
+PACK = 4
+PASSES = CHANNELS // (P * PACK)
+
+PITCH = GRID + 1
+PLANE = GRID * PITCH
+LEAD = 2 * PITCH + 1
+ROW = LEAD + PLANE + 1
+
+OFFSETS = [(di, dj) for di in (-2, -1) for dj in (-1, 0, 1)] + [(0, -1)]
+CENTRE = len(OFFSETS)
+WINDOW = 9
+
+EPS_CUBED = 1e-18
+FLOOR_SQUARED = 1e-24
+LN_SMALLEST = 1e-18
+
+SECOND = (0, PLANE - P)
+TOKEN_PAD = 2 * P
+STORE_GROUP = 8
+
+FLOPS = 2 * IMAGES * TOKENS * CHANNELS * FEATURES
+
+
+def tile_tokenmudule_pa_t_kernel(tc, patch_tokens, fc1_w, fc1_b, out):
+    nc = tc.nc
+    with ExitStack() as ctx:
+        const = ctx.enter_context(tc.tile_pool(name="const", bufs=1))
+        loads = ctx.enter_context(tc.tile_pool(name="loads", bufs=3))
+        rows = ctx.enter_context(tc.tile_pool(name="rows", bufs=1))
+        small = ctx.enter_context(tc.tile_pool(name="small", bufs=3))
+        psum_x = ctx.enter_context(tc.psum_pool(name="psum_x", bufs=2))
+        psum_r = ctx.enter_context(tc.psum_pool(name="psum_r", bufs=4))
+        psum_s = ctx.enter_context(tc.psum_pool(name="psum_s", bufs=1))
+        psum_m = ctx.enter_context(tc.psum_pool(name="psum_m", bufs=1))
+
+        ident_bf = const.tile([P, P], BF16, name="ident_bf")
+        make_identity(nc, ident_bf[:])
+        ident_f32 = const.tile([P, P], F32, name="ident_f32")
+        make_identity(nc, ident_f32[:])
+        ones = const.tile([P, P], F32, name="ones")
+        nc.vector.memset(ones[:], 1.0)
+
+        bias_bf = const.tile([P, FEATURES], BF16, name="bias_bf")
+        nc.sync.dma_start(out=bias_bf[:], in_=fc1_b.partition_broadcast(P))
+        bias = const.tile([P, FEATURES], F32, name="bias")
+        nc.vector.tensor_copy(out=bias[:], in_=bias_bf[:])
+
+        w_raw = const.tile([P, BLOCKS, FEATURES], BF16, name="w_raw")
+        nc.sync.dma_start(out=w_raw[:], in_=fc1_w.rearrange("(a p) n -> p a n", p=P))
+        w_grouped = const.tile([P, PASSES, FEATURES, PACK], BF16, name="w_grouped", align_bytes=64)
+        for g in range(PASSES):
+            nc.vector.tensor_copy(
+                out=w_grouped[:, g, :, :], in_=w_raw[:, PACK * g : PACK * (g + 1), :].rearrange("p t n -> p n t")
+            )
+        w_codes = const.tile([P, PASSES * FEATURES], U32, name="w_codes", align_bytes=64)
+        w_scales = const.tile([P, PASSES * FEATURES], U8, name="w_scales", align_bytes=64)
+        nc.vector.quantize_mx(
+            out=w_codes[:].bitcast(FP8X4),
+            scales=w_scales[:],
+            in_=w_grouped[:].rearrange("p g n t -> p (g n t)"),
+        )
+
+        X_RING = 5
+        x_ring = [const.tile([P, BLOCKS, ROW], BF16, name="x_pad%d" % n) for n in range(X_RING)]
+        for x_pad in x_ring:
+            nc.vector.memset(x_pad[:], 0.0)
+        G_RING = 2
+        g_ring = [
+            const.tile([P, PASSES, TOKEN_PAD, PACK], BF16, name="grouped%d" % n, align_bytes=64)
+            for n in range(G_RING)
+        ]
+        for grouped in g_ring:
+            nc.vector.memset(grouped[:], 0.0)
+        JUNK = 4
+        junk_row = const.tile([P, JUNK, ROW], BF16, name="junk_row")
+        junk_bank = const.tile([P, JUNK, 512], BF16, name="junk_bank")
+
+        tiles = {}
+
+        def grid_of(plane_ap):
+            return plane_ap.rearrange("p k (i j) -> p k i j", j=PITCH)[:, :, :, 0:GRID]
+
+        def load(b):
+            x_in = loads.tile([P, 2, CHANNELS], BF16, name="x_in")
+            nc.sync.dma_start(out=x_in[:, 0, :], in_=patch_tokens[b, 0:P, :])
+            nc.sync.dma_start(out=x_in[:, 1, :], in_=patch_tokens[b, TOKENS - P : TOKENS, :])
+            tiles["x_in", b] = x_in
+
+        def transpose_in(b):
+            x_in = tiles["x_in", b]
+            x_pad = x_ring[b % X_RING]
+            half = BLOCKS // 2
+            for h in range(2):
+                x_t = psum_x.tile([P, half, TOKENS], BF16, name="x_t")
+                for kk in range(half):
+                    cols = slice((half * h + kk) * P, (half * h + kk + 1) * P)
+                    nc.tensor.transpose(x_t[:, kk, 0:P], x_in[:, 0, cols], ident_bf[:])
+                    nc.tensor.transpose(x_t[:, kk, TOKENS - P : TOKENS], x_in[:, 1, cols], ident_bf[:])
+                nc.scalar.copy(
+                    out=grid_of(x_pad[:, half * h : half * (h + 1), LEAD : LEAD + PLANE]),
+                    in_=x_t[:].rearrange("p k (i j) -> p k i j", j=GRID),
+                )
+            square = rows.tile([P, BLOCKS, ROW], F32, name="square")
+            sum_sq = small.tile([P, BLOCKS], F32, name="sum_sq")
+            norm_sq = small.tile([P, BLOCKS, CENTRE + 1], F32, name="norm_sq", bufs=4)
+            for k in range(BLOCKS):
+                nc.scalar.activation(
+                    out=square[:, k, :], in_=x_pad[:, k, :], func=ACT.Square, accum_out=sum_sq[:, k : k + 1]
+                )
+            for k in range(BLOCKS):
+                nc.scalar.activation(
+                    out=junk_row[:, k % JUNK, :],
+                    in_=square[:, k, :],
+                    func=ACT.Square,
+                    accum_out=norm_sq[:, k, CENTRE : CENTRE + 1],
+                )
+            mean_sq = small.tile([P, BLOCKS], F32, name="mean_sq")
+            nc.gpsimd.tensor_scalar(
+                out=mean_sq[:], in0=sum_sq[:], scalar1=1.0 / TOKENS, scalar2=1e-20, op0=ALU.mult, op1=ALU.max
+            )
+            tiles["square", b] = square
+            tiles["norm_sq", b] = norm_sq
+            tiles["mean_sq", b] = mean_sq
+
+        def row_scale(b):
+            c = small.tile([P, BLOCKS], F32, name="c", bufs=5)
+            nc.vector.reciprocal(out=c[:], in_=tiles["mean_sq", b][:])
+            tiles["c", b] = c
+
+        def cubes(b):
+            x_pad = x_ring[b % X_RING]
+            cube = rows.tile([P, BLOCKS, ROW], F32, name="cube", bufs=3)
+            for k in range(BLOCKS):
+                nc.vector.scalar_tensor_tensor(
+                    out=cube[:, k, :],
+                    in0=x_pad[:, k, :],
+                    scalar=tiles["c", b][:, k : k + 1],
+                    in1=tiles["square", b][:, k, :],
+                    op0=ALU.mult,
+                    op1=ALU.mult,
+                )
+            tiles["cube", b] = cube
+
+        def window_norms(b):
+            x_pad = x_ring[b % X_RING]
+            norm_sq = tiles["norm_sq", b]
+            for o, (di, dj) in enumerate(OFFSETS):
+                first = LEAD - PITCH * di
+                shift = PITCH * di + dj
+                length = PLANE + PITCH * di
+                z = rows.tile([P, BLOCKS, PLANE], F32, name="z", bufs=4)
+                nc.vector.tensor_tensor(
+                    out=z[:, :, 0:length],
+                    in0=x_pad[:, :, first : first + length],
+                    in1=x_pad[:, :, first + shift : first + shift + length],
+                    op=ALU.mult,
+                )
+                for k in range(BLOCKS):
+                    nc.scalar.activation(
+                        out=z[:, k, 0:length],
+                        in_=z[:, k, 0:length],
+                        func=ACT.Square,
+                        accum_out=norm_sq[:, k, o : o + 1],
+                    )
+
+        def scaled_norms(b):
+            c_wide = tiles["c", b][:].unsqueeze(2).to_broadcast([P, BLOCKS, CENTRE + 1])
+            scaled = small.tile([P, BLOCKS, CENTRE + 1], F32, name="scaled")
+            nc.gpsimd.tensor_scalar(
+                out=scaled[:], in0=tiles["norm_sq", b][:], scalar1=FLOOR_SQUARED, scalar2=None, op0=ALU.max
+            )
+            nc.gpsimd.tensor_tensor(out=scaled[:], in0=scaled[:], in1=c_wide, op=ALU.mult)
+            nc.gpsimd.tensor_tensor(out=scaled[:], in0=scaled[:], in1=c_wide, op=ALU.mult)
+            nc.gpsimd.tensor_scalar(
+                out=scaled[:], in0=scaled[:], scalar1=LN_SMALLEST, scalar2=None, op0=ALU.max
+            )
+            tiles["scaled", b] = scaled
+
+        def weights_ln(b):
+            nc.scalar.activation(out=tiles["scaled", b][:], in_=tiles["scaled", b][:], func=ACT.Ln)
+
+        def weights_exp(b):
+            ln_scaled = tiles["scaled", b]
+            power = small.tile([P, BLOCKS, CENTRE + 1], F32, name="power")
+            nc.scalar.activation(out=power[:], in_=ln_scaled[:], func=ACT.Exp, scale=-1.5)
+            centre_scale = small.tile([P, BLOCKS], F32, name="centre_scale")
+            nc.scalar.activation(out=centre_scale[:], in_=ln_scaled[:, :, CENTRE], func=ACT.Exp, scale=-0.75)
+            weight = small.tile([P, BLOCKS, CENTRE + 1], F32, name="weight")
+            nc.gpsimd.tensor_tensor(
+                out=weight[:],
+                in0=power[:],
+                in1=tiles["c", b][:].unsqueeze(2).to_broadcast([P, BLOCKS, CENTRE + 1]),
+                op=ALU.mult,
+            )
+            tiles["centre_scale", b] = centre_scale
+            tiles["weight", b] = weight
+
+        def centre_term(b):
+            centre = rows.tile([P, BLOCKS, PLANE], F32, name="centre")
+            for k in range(BLOCKS):
+                nc.scalar.activation(
+                    out=centre[:, k, :],
+                    in_=tiles["cube", b][:, k, LEAD : LEAD + PLANE],
+                    func=ACT.Square,
+                    scale=tiles["centre_scale", b][:, k : k + 1],
+                )
+            tiles["centre", b] = centre
+
+        def pool_terms(b):
+            cube = tiles["cube", b]
+            weight = tiles["weight", b]
+            total = rows.tile([P, BLOCKS, PLANE], F32, name="total", bufs=3)
+            tiles["total", b] = total
+
+            def products(o):
+                di, dj = OFFSETS[o]
+                first = LEAD - PITCH * di
+                shift = PITCH * di + dj
+                length = PLANE + PITCH * di
+                u_cubed = rows.tile([P, BLOCKS, PLANE], F32, name="u_cubed", bufs=3)
+                for k in range(BLOCKS):
+                    nc.vector.scalar_tensor_tensor(
+                        out=u_cubed[:, k, 0:length],
+                        in0=cube[:, k, first + shift : first + shift + length],
+                        scalar=weight[:, k, o : o + 1],
+                        in1=cube[:, k, first : first + length],
+                        op0=ALU.mult,
+                        op1=ALU.mult,
+                    )
+                return u_cubed
+
+            def add_terms(term_ap, total_ap):
+                nc.vector.scalar_tensor_tensor(
+                    out=total_ap, in0=term_ap, scalar=EPS_CUBED, in1=total_ap, op0=ALU.max, op1=ALU.add
+                )
+
+            def add_offset(o, u_cubed):
+                di, dj = OFFSETS[o]
+                length = PLANE + PITCH * di
+                add_terms(u_cubed[:, :, 0:length], total[:, :, PLANE - length : PLANE])
+                if di == 0:
+                    add_terms(u_cubed[:, :, 1:PLANE], total[:, :, 0 : PLANE - 1])
+
+            for k in range(BLOCKS):
+                nc.vector.tensor_scalar(
+                    out=total[:, k, :],
+                    in0=tiles["centre", b][:, k, :],
+                    scalar1=tiles["c", b][:, k : k + 1],
+                    scalar2=EPS_CUBED,
+                    op0=ALU.mult,
+                    op1=ALU.max,
+                )
+            waiting = products(0)
+            for line in range(2):
+                missing = 3 * (2 - line)
+                nc.vector.tensor_scalar(
+                    out=total[:, :, PITCH * line : PITCH * (line + 1)],
+                    in0=total[:, :, PITCH * line : PITCH * (line + 1)],
+                    scalar1=missing * EPS_CUBED,
+                    scalar2=None,
+                    op0=ALU.add,
+                )
+            for o in range(1, len(OFFSETS)):
+                u_cubed = products(o)
+                add_offset(o - 1, waiting)
+                waiting = u_cubed
+            add_offset(len(OFFSETS) - 1, waiting)
+
+        def root_ln(b):
+            flat = tiles["total", b][:].rearrange("p k e -> p (k e)")
+            nc.scalar.activation(out=flat, in_=flat, func=ACT.Ln, scale=1.0 / WINDOW)
+
+        def root_exp(b):
+            flat = tiles["total", b][:].rearrange("p k e -> p (k e)")
+            nc.scalar.activation(out=flat, in_=flat, func=ACT.Exp, scale=1.0 / 3.0)
+
+        def residual(b):
+            r = tiles["total", b]
+            x_pad = x_ring[b % X_RING]
+            nc.vector.tensor_tensor(out=r[:], in0=r[:], in1=x_pad[:, :, LEAD : LEAD + PLANE], op=ALU.add)
+            half = BLOCKS // 2
+            for w in range(2):
+                for h in range(2):
+                    r_t = psum_r.tile([P, half, P], F32, name="r_t")
+                    for kk in range(half):
+                        nc.tensor.transpose(
+                            r_t[:, kk, :], r[:, half * h + kk, SECOND[w] : SECOND[w] + P], ident_f32[:]
+                        )
+                    tiles["r_t", b, w, h] = r_t
+
+        def token_norms(b):
+            parts = small.tile([P, 2, 2], F32, name="parts")
+            for w in range(2):
+                for h in range(2):
+                    nc.scalar.activation(
+                        out=junk_bank[:, 2 * w + h, :],
+                        in_=tiles["r_t", b, w, h][:].rearrange("p k c -> p (k c)"),
+                        func=ACT.Square,
+                        accum_out=parts[:, w, h : h + 1],
+                    )
+            length_sq = small.tile([P, 2], F32, name="length_sq")
+            nc.gpsimd.tensor_tensor(out=length_sq[:], in0=parts[:, :, 0], in1=parts[:, :, 1], op=ALU.add)
+            nc.gpsimd.tensor_scalar(
+                out=length_sq[:], in0=length_sq[:], scalar1=FLOOR_SQUARED, scalar2=None, op0=ALU.max
+            )
+            tiles["length_sq", b] = length_sq
+
+        def length_ln(b):
+            ln_length = small.tile([P, 2], F32, name="ln_length")
+            nc.scalar.activation(out=ln_length[:], in_=tiles["length_sq", b][:], func=ACT.Ln)
+            tiles["ln_length", b] = ln_length
+
+        def length_exp(b):
+            a = tiles["length_sq", b]
+            y = small.tile([P, 2], F32, name="y")
+            nc.scalar.activation(out=y[:], in_=tiles["ln_length", b][:], func=ACT.Exp, scale=-0.5)
+            step = small.tile([P, 2], F32, name="step")
+            nc.gpsimd.tensor_tensor(out=step[:], in0=a[:], in1=y[:], op=ALU.mult)
+            nc.gpsimd.tensor_tensor(out=step[:], in0=step[:], in1=y[:], op=ALU.mult)
+            nc.gpsimd.tensor_scalar(
+                out=step[:], in0=step[:], scalar1=-0.5, scalar2=1.5, op0=ALU.mult, op1=ALU.add
+            )
+            inverse = small.tile([P, 2], F32, name="inverse")
+            nc.gpsimd.tensor_tensor(out=inverse[:], in0=y[:], in1=step[:], op=ALU.mult)
+            tiles["inverse", b] = inverse
+
+        def spread_inverse(b):
+            repeated = small.tile([P, 2, P], F32, name="repeated", bufs=2)
+            spread = psum_s.tile([P, PLANE], F32, name="spread")
+            for w in range(2):
+                nc.scalar.activation(
+                    out=repeated[:, w, :], in_=ones[:], func=ACT.Copy, scale=tiles["inverse", b][:, w : w + 1]
+                )
+                nc.tensor.transpose(spread[:, SECOND[w] : SECOND[w] + P], repeated[:, w, :], ident_f32[:])
+            tiles["spread", b] = spread
+
+        def normalise(b):
+            r = tiles["total", b]
+            grouped = g_ring[b % G_RING]
+            spread = tiles["spread", b][:].rearrange("p (i j) -> p i j", j=PITCH)[:, :, 0:GRID]
+            for g in range(PASSES):
+                nc.vector.tensor_tensor(
+                    out=grouped[:, g, 0:TOKENS, :].rearrange("p (i j) t -> p i j t", j=GRID),
+                    in0=r[:, PACK * g : PACK * (g + 1), :].rearrange("p t (i j) -> p i j t", j=PITCH)[
+                        :, :, 0:GRID, :
+                    ],
+                    in1=spread.unsqueeze(3).to_broadcast([P, GRID, GRID, PACK]),
+                    op=ALU.mult,
+                )
+
+        def project(b):
+            grouped = g_ring[b % G_RING]
+            codes = small.tile([P, PASSES * TOKEN_PAD], U32, name="codes", bufs=2, align_bytes=64)
+            scales = small.tile([P, PASSES * TOKEN_PAD], U8, name="scales", bufs=2, align_bytes=64)
+            nc.vector.quantize_mx(
+                out=codes[:].bitcast(FP8X4), scales=scales[:], in_=grouped[:].rearrange("p g n t -> p (g n t)")
+            )
+            product = psum_m.tile([P, 2, FEATURES], F32, name="product")
+            for m in range(2):
+                for g in range(PASSES):
+                    token_cols = slice(g * TOKEN_PAD + m * P, g * TOKEN_PAD + (m + 1) * P)
+                    w_cols = slice(g * FEATURES, (g + 1) * FEATURES)
+                    nc.tensor.matmul_mx(
+                        out=product[:, m, :],
+                        lhsT=codes[:, token_cols].bitcast(FP8X4),
+                        lhsT_scale=scales[:, token_cols],
+                        rhs=w_codes[:, w_cols].bitcast(FP8X4),
+                        rhs_scale=w_scales[:, w_cols],
+                        start=(g == 0),
+                        stop=(g == PASSES - 1),
+                    )
+            tiles["product", b] = product
+
+        def finish(b):
+            n = b % STORE_GROUP
+            if n == 0:
+                tiles["result"] = rows.tile([P, STORE_GROUP, 2, FEATURES], F32, name="result", bufs=2)
+            result = tiles["result"]
+            nc.vector.tensor_tensor(
+                out=result[:, n, :, :],
+                in0=tiles["product", b][:],
+                in1=bias[:].unsqueeze(1).to_broadcast([P, 2, FEATURES]),
+                op=ALU.add,
+            )
+            if n == STORE_GROUP - 1:
+                flat = result[:].rearrange("p n m f -> p (n m f)")
+                nc.scalar.activation(out=flat, in_=flat, func=ACT.Gelu)
+                nc.sync.dma_start(
+                    out=out[b - n : b + 1, 0:P, :].rearrange("n t f -> t n f"), in_=result[:, :, 0, :]
+                )
+                nc.sync.dma_start(
+                    out=out[b - n : b + 1, P:TOKENS, :].rearrange("n t f -> t n f"),
+                    in_=result[0 : TOKENS - P, :, 1, :],
+                )
+
+        def when_valid(stage, b):
+            if 0 <= b < IMAGES:
+                stage(b)
+
+        with tc.manual_schedule():
+            load(0)
+            load(1)
+            LAST_STAGE = 7
+            for i in range(IMAGES + LAST_STAGE):
+                when_valid(normalise, i - 6)
+                when_valid(finish, i - 7)
+                when_valid(project, i - 6)
+                when_valid(load, i + 2)
+                when_valid(token_norms, i - 5)
+                when_valid(scaled_norms, i - 2)
+                when_valid(root_ln, i - 4)
+                when_valid(weights_ln, i - 2)
+                when_valid(length_ln, i - 5)
+                when_valid(root_exp, i - 4)
+                when_valid(weights_exp, i - 2)
+                when_valid(length_exp, i - 5)
+                when_valid(pool_terms, i - 3)
+                when_valid(centre_term, i - 2)
+                when_valid(transpose_in, i)
+                when_valid(spread_inverse, i - 5)
+                when_valid(window_norms, i - 1)
+                when_valid(row_scale, i)
+                when_valid(residual, i - 4)
+                when_valid(cubes, i)

@@ -22,9 +22,8 @@ PACK = 4
 PASSES = CHANNELS // (P * PACK)
 
 PITCH = GRID + 1
-PLANE = GRID * PITCH
 LEAD = 2 * PITCH + 1
-ROW = LEAD + PLANE + 1
+ROW = LEAD + (GRID + 1) * PITCH
 
 OFFSETS = [(di, dj) for di in (-2, -1) for dj in (-1, 0, 1)] + [(0, -1)]
 CENTRE = len(OFFSETS)
@@ -34,7 +33,7 @@ EPS_CUBED = 1e-18
 FLOOR_SQUARED = 1e-24
 LN_SMALLEST = 1e-18
 
-SECOND = (0, PLANE - P)
+WINDOW_START = (0, TOKENS - P)
 TOKEN_PAD = 2 * P
 STORE_GROUP = 8
 
@@ -59,6 +58,12 @@ def tile_tokenmudule_pa_t_kernel(tc, patch_tokens, fc1_w, fc1_b, out):
         make_identity(nc, ident_f32[:])
         ones = const.tile([P, P], F32, name="ones")
         nc.vector.memset(ones[:], 1.0)
+        ln_smallest = const.tile([P, 1], F32, name="ln_smallest")
+        nc.vector.memset(ln_smallest[:], LN_SMALLEST)
+        floor_plus = const.tile([P, 1], F32, name="floor_plus")
+        nc.vector.memset(floor_plus[:], FLOOR_SQUARED)
+        floor_minus = const.tile([P, 1], F32, name="floor_minus")
+        nc.vector.memset(floor_minus[:], -FLOOR_SQUARED)
 
         bias_bf = const.tile([P, FEATURES], BF16, name="bias_bf")
         nc.sync.dma_start(out=bias_bf[:], in_=fc1_b.partition_broadcast(P))
@@ -80,7 +85,7 @@ def tile_tokenmudule_pa_t_kernel(tc, patch_tokens, fc1_w, fc1_b, out):
             in_=w_grouped[:].rearrange("p g n t -> p (g n t)"),
         )
 
-        X_RING = 5
+        X_RING = 4
         x_ring = [const.tile([P, BLOCKS, ROW], BF16, name="x_pad%d" % n) for n in range(X_RING)]
         for x_pad in x_ring:
             nc.vector.memset(x_pad[:], 0.0)
@@ -97,13 +102,22 @@ def tile_tokenmudule_pa_t_kernel(tc, patch_tokens, fc1_w, fc1_b, out):
 
         tiles = {}
 
-        def grid_of(plane_ap):
-            return plane_ap.rearrange("p k (i j) -> p k i j", j=PITCH)[:, :, :, 0:GRID]
+        def lines_of_rows(padded, first_line, n_lines, shift):
+            start = LEAD + PITCH * first_line + shift
+            view = padded[:, :, start : start + PITCH * n_lines]
+            return view.rearrange("p k (i j) -> p k i j", j=PITCH)[:, :, :, 0:GRID]
+
+        def lines_of_row(padded, k, first_line, n_lines, shift):
+            start = LEAD + PITCH * first_line + shift
+            view = padded[:, k, start : start + PITCH * n_lines]
+            return view.rearrange("p (i j) -> p i j", j=PITCH)[:, :, 0:GRID]
 
         def load(b):
             x_in = loads.tile([P, 2, CHANNELS], BF16, name="x_in")
-            nc.sync.dma_start(out=x_in[:, 0, :], in_=patch_tokens[b, 0:P, :])
-            nc.sync.dma_start(out=x_in[:, 1, :], in_=patch_tokens[b, TOKENS - P : TOKENS, :])
+            for w in range(2):
+                nc.sync.dma_start(
+                    out=x_in[:, w, :], in_=patch_tokens[b, WINDOW_START[w] : WINDOW_START[w] + P, :]
+                )
             tiles["x_in", b] = x_in
 
         def transpose_in(b):
@@ -114,15 +128,17 @@ def tile_tokenmudule_pa_t_kernel(tc, patch_tokens, fc1_w, fc1_b, out):
                 x_t = psum_x.tile([P, half, TOKENS], BF16, name="x_t")
                 for kk in range(half):
                     cols = slice((half * h + kk) * P, (half * h + kk + 1) * P)
-                    nc.tensor.transpose(x_t[:, kk, 0:P], x_in[:, 0, cols], ident_bf[:])
-                    nc.tensor.transpose(x_t[:, kk, TOKENS - P : TOKENS], x_in[:, 1, cols], ident_bf[:])
+                    for w in range(2):
+                        nc.tensor.transpose(
+                            x_t[:, kk, WINDOW_START[w] : WINDOW_START[w] + P], x_in[:, w, cols], ident_bf[:]
+                        )
                 nc.scalar.copy(
-                    out=grid_of(x_pad[:, half * h : half * (h + 1), LEAD : LEAD + PLANE]),
+                    out=lines_of_rows(x_pad[:, half * h : half * (h + 1), :], 0, GRID, 0),
                     in_=x_t[:].rearrange("p k (i j) -> p k i j", j=GRID),
                 )
-            square = rows.tile([P, BLOCKS, ROW], F32, name="square")
+            square = rows.tile([P, BLOCKS, ROW], F32, name="square", bufs=2)
             sum_sq = small.tile([P, BLOCKS], F32, name="sum_sq")
-            norm_sq = small.tile([P, BLOCKS, CENTRE + 1], F32, name="norm_sq", bufs=4)
+            norm_sq = small.tile([P, BLOCKS, CENTRE + 1], F32, name="norm_sq")
             for k in range(BLOCKS):
                 nc.scalar.activation(
                     out=square[:, k, :], in_=x_pad[:, k, :], func=ACT.Square, accum_out=sum_sq[:, k : k + 1]
@@ -134,22 +150,33 @@ def tile_tokenmudule_pa_t_kernel(tc, patch_tokens, fc1_w, fc1_b, out):
                     func=ACT.Square,
                     accum_out=norm_sq[:, k, CENTRE : CENTRE + 1],
                 )
-            mean_sq = small.tile([P, BLOCKS], F32, name="mean_sq")
-            nc.gpsimd.tensor_scalar(
-                out=mean_sq[:], in0=sum_sq[:], scalar1=1.0 / TOKENS, scalar2=1e-20, op0=ALU.mult, op1=ALU.max
-            )
             tiles["square", b] = square
+            tiles["sum_sq", b] = sum_sq
             tiles["norm_sq", b] = norm_sq
+
+        def mean_square(b):
+            mean_sq = small.tile([P, BLOCKS], F32, name="mean_sq")
+            nc.vector.tensor_scalar(
+                out=mean_sq[:],
+                in0=tiles["sum_sq", b][:],
+                scalar1=1.0 / TOKENS,
+                scalar2=1e-20,
+                op0=ALU.mult,
+                op1=ALU.max,
+            )
             tiles["mean_sq", b] = mean_sq
 
         def row_scale(b):
-            c = small.tile([P, BLOCKS], F32, name="c", bufs=5)
+            c = small.tile([P, BLOCKS], F32, name="c")
             nc.vector.reciprocal(out=c[:], in_=tiles["mean_sq", b][:])
             tiles["c", b] = c
 
+        def c_for_offsets(b):
+            return tiles["c", b][:].unsqueeze(2).to_broadcast([P, BLOCKS, CENTRE + 1])
+
         def cubes(b):
             x_pad = x_ring[b % X_RING]
-            cube = rows.tile([P, BLOCKS, ROW], F32, name="cube", bufs=3)
+            cube = rows.tile([P, BLOCKS, ROW], F32, name="cube", bufs=2)
             for k in range(BLOCKS):
                 nc.vector.scalar_tensor_tensor(
                     out=cube[:, k, :],
@@ -165,14 +192,13 @@ def tile_tokenmudule_pa_t_kernel(tc, patch_tokens, fc1_w, fc1_b, out):
             x_pad = x_ring[b % X_RING]
             norm_sq = tiles["norm_sq", b]
             for o, (di, dj) in enumerate(OFFSETS):
-                first = LEAD - PITCH * di
-                shift = PITCH * di + dj
-                length = PLANE + PITCH * di
-                z = rows.tile([P, BLOCKS, PLANE], F32, name="z", bufs=4)
+                n_lines = GRID + di
+                length = GRID * n_lines
+                z = rows.tile([P, BLOCKS, TOKENS], F32, name="z", bufs=len(OFFSETS))
                 nc.vector.tensor_tensor(
-                    out=z[:, :, 0:length],
-                    in0=x_pad[:, :, first : first + length],
-                    in1=x_pad[:, :, first + shift : first + shift + length],
+                    out=z[:, :, 0:length].rearrange("p k (i j) -> p k i j", j=GRID),
+                    in0=lines_of_rows(x_pad, -di, n_lines, 0),
+                    in1=lines_of_rows(x_pad, -di, n_lines, PITCH * di + dj),
                     op=ALU.mult,
                 )
                 for k in range(BLOCKS):
@@ -183,21 +209,25 @@ def tile_tokenmudule_pa_t_kernel(tc, patch_tokens, fc1_w, fc1_b, out):
                         accum_out=norm_sq[:, k, o : o + 1],
                     )
 
-        def scaled_norms(b):
-            c_wide = tiles["c", b][:].unsqueeze(2).to_broadcast([P, BLOCKS, CENTRE + 1])
+        def scaled_norms_first(b):
             scaled = small.tile([P, BLOCKS, CENTRE + 1], F32, name="scaled")
-            nc.gpsimd.tensor_scalar(
-                out=scaled[:], in0=tiles["norm_sq", b][:], scalar1=FLOOR_SQUARED, scalar2=None, op0=ALU.max
-            )
-            nc.gpsimd.tensor_tensor(out=scaled[:], in0=scaled[:], in1=c_wide, op=ALU.mult)
-            nc.gpsimd.tensor_tensor(out=scaled[:], in0=scaled[:], in1=c_wide, op=ALU.mult)
-            nc.gpsimd.tensor_scalar(
-                out=scaled[:], in0=scaled[:], scalar1=LN_SMALLEST, scalar2=None, op0=ALU.max
+            nc.vector.scalar_tensor_tensor(
+                out=scaled[:],
+                in0=tiles["norm_sq", b][:],
+                scalar=FLOOR_SQUARED,
+                in1=c_for_offsets(b),
+                op0=ALU.max,
+                op1=ALU.mult,
             )
             tiles["scaled", b] = scaled
 
+        def scaled_norms_second(b):
+            scaled = tiles["scaled", b]
+            nc.vector.tensor_tensor(out=scaled[:], in0=scaled[:], in1=c_for_offsets(b), op=ALU.mult)
+
         def weights_ln(b):
-            nc.scalar.activation(out=tiles["scaled", b][:], in_=tiles["scaled", b][:], func=ACT.Ln)
+            scaled = tiles["scaled", b]
+            nc.scalar.activation(out=scaled[:], in_=scaled[:], func=ACT.Ln, bias=ln_smallest[:])
 
         def weights_exp(b):
             ln_scaled = tiles["scaled", b]
@@ -205,22 +235,20 @@ def tile_tokenmudule_pa_t_kernel(tc, patch_tokens, fc1_w, fc1_b, out):
             nc.scalar.activation(out=power[:], in_=ln_scaled[:], func=ACT.Exp, scale=-1.5)
             centre_scale = small.tile([P, BLOCKS], F32, name="centre_scale")
             nc.scalar.activation(out=centre_scale[:], in_=ln_scaled[:, :, CENTRE], func=ACT.Exp, scale=-0.75)
-            weight = small.tile([P, BLOCKS, CENTRE + 1], F32, name="weight")
-            nc.gpsimd.tensor_tensor(
-                out=weight[:],
-                in0=power[:],
-                in1=tiles["c", b][:].unsqueeze(2).to_broadcast([P, BLOCKS, CENTRE + 1]),
-                op=ALU.mult,
-            )
+            tiles["power", b] = power
             tiles["centre_scale", b] = centre_scale
+
+        def weights(b):
+            weight = small.tile([P, BLOCKS, CENTRE + 1], F32, name="weight")
+            nc.vector.tensor_tensor(out=weight[:], in0=tiles["power", b][:], in1=c_for_offsets(b), op=ALU.mult)
             tiles["weight", b] = weight
 
         def centre_term(b):
-            centre = rows.tile([P, BLOCKS, PLANE], F32, name="centre")
+            centre = rows.tile([P, BLOCKS, TOKENS], F32, name="centre")
             for k in range(BLOCKS):
                 nc.scalar.activation(
-                    out=centre[:, k, :],
-                    in_=tiles["cube", b][:, k, LEAD : LEAD + PLANE],
+                    out=centre[:, k, :].rearrange("p (i j) -> p i j", j=GRID),
+                    in_=lines_of_row(tiles["cube", b], k, 0, GRID, 0),
                     func=ACT.Square,
                     scale=tiles["centre_scale", b][:, k : k + 1],
                 )
@@ -229,21 +257,19 @@ def tile_tokenmudule_pa_t_kernel(tc, patch_tokens, fc1_w, fc1_b, out):
         def pool_terms(b):
             cube = tiles["cube", b]
             weight = tiles["weight", b]
-            total = rows.tile([P, BLOCKS, PLANE], F32, name="total", bufs=3)
+            total = rows.tile([P, BLOCKS, TOKENS], F32, name="total", bufs=3)
             tiles["total", b] = total
 
             def products(o):
                 di, dj = OFFSETS[o]
-                first = LEAD - PITCH * di
-                shift = PITCH * di + dj
-                length = PLANE + PITCH * di
-                u_cubed = rows.tile([P, BLOCKS, PLANE], F32, name="u_cubed", bufs=3)
+                n_lines = GRID + di if di < 0 else GRID + 1
+                u_cubed = rows.tile([P, BLOCKS, (GRID + 1) * GRID], F32, name="u_cubed", bufs=3)
                 for k in range(BLOCKS):
                     nc.vector.scalar_tensor_tensor(
-                        out=u_cubed[:, k, 0:length],
-                        in0=cube[:, k, first + shift : first + shift + length],
+                        out=u_cubed[:, k, 0 : GRID * n_lines].rearrange("p (i j) -> p i j", j=GRID),
+                        in0=lines_of_row(cube, k, -di, n_lines, PITCH * di + dj),
                         scalar=weight[:, k, o : o + 1],
-                        in1=cube[:, k, first : first + length],
+                        in1=lines_of_row(cube, k, -di, n_lines, 0),
                         op0=ALU.mult,
                         op1=ALU.mult,
                     )
@@ -256,11 +282,12 @@ def tile_tokenmudule_pa_t_kernel(tc, patch_tokens, fc1_w, fc1_b, out):
 
             def add_offset(o, u_cubed):
                 di, dj = OFFSETS[o]
-                length = PLANE + PITCH * di
-                add_terms(u_cubed[:, :, 0:length], total[:, :, PLANE - length : PLANE])
+                length = GRID * (GRID + di)
+                add_terms(u_cubed[:, :, 0:length], total[:, :, TOKENS - length : TOKENS])
                 if di == 0:
-                    add_terms(u_cubed[:, :, 1:PLANE], total[:, :, 0 : PLANE - 1])
+                    add_terms(u_cubed[:, :, 1 : TOKENS + 1], total[:, :, :])
 
+            waiting = products(0)
             for k in range(BLOCKS):
                 nc.vector.tensor_scalar(
                     out=total[:, k, :],
@@ -270,18 +297,18 @@ def tile_tokenmudule_pa_t_kernel(tc, patch_tokens, fc1_w, fc1_b, out):
                     op0=ALU.mult,
                     op1=ALU.max,
                 )
-            waiting = products(0)
-            for line in range(2):
-                missing = 3 * (2 - line)
-                nc.vector.tensor_scalar(
-                    out=total[:, :, PITCH * line : PITCH * (line + 1)],
-                    in0=total[:, :, PITCH * line : PITCH * (line + 1)],
-                    scalar1=missing * EPS_CUBED,
-                    scalar2=None,
-                    op0=ALU.add,
-                )
             for o in range(1, len(OFFSETS)):
                 u_cubed = products(o)
+                if o == 1:
+                    for line in range(2):
+                        missing = 3 * (2 - line)
+                        nc.vector.tensor_scalar(
+                            out=total[:, :, GRID * line : GRID * (line + 1)],
+                            in0=total[:, :, GRID * line : GRID * (line + 1)],
+                            scalar1=missing * EPS_CUBED,
+                            scalar2=None,
+                            op0=ALU.add,
+                        )
                 add_offset(o - 1, waiting)
                 waiting = u_cubed
             add_offset(len(OFFSETS) - 1, waiting)
@@ -296,15 +323,19 @@ def tile_tokenmudule_pa_t_kernel(tc, patch_tokens, fc1_w, fc1_b, out):
 
         def residual(b):
             r = tiles["total", b]
-            x_pad = x_ring[b % X_RING]
-            nc.vector.tensor_tensor(out=r[:], in0=r[:], in1=x_pad[:, :, LEAD : LEAD + PLANE], op=ALU.add)
+            grid = r[:].rearrange("p k (i j) -> p k i j", j=GRID)
+            nc.vector.tensor_tensor(
+                out=grid, in0=grid, in1=lines_of_rows(x_ring[b % X_RING], 0, GRID, 0), op=ALU.add
+            )
             half = BLOCKS // 2
             for w in range(2):
                 for h in range(2):
                     r_t = psum_r.tile([P, half, P], F32, name="r_t")
                     for kk in range(half):
                         nc.tensor.transpose(
-                            r_t[:, kk, :], r[:, half * h + kk, SECOND[w] : SECOND[w] + P], ident_f32[:]
+                            r_t[:, kk, :],
+                            r[:, half * h + kk, WINDOW_START[w] : WINDOW_START[w] + P],
+                            ident_f32[:],
                         )
                     tiles["r_t", b, w, h] = r_t
 
@@ -319,52 +350,45 @@ def tile_tokenmudule_pa_t_kernel(tc, patch_tokens, fc1_w, fc1_b, out):
                         accum_out=parts[:, w, h : h + 1],
                     )
             length_sq = small.tile([P, 2], F32, name="length_sq")
-            nc.gpsimd.tensor_tensor(out=length_sq[:], in0=parts[:, :, 0], in1=parts[:, :, 1], op=ALU.add)
-            nc.gpsimd.tensor_scalar(
-                out=length_sq[:], in0=length_sq[:], scalar1=FLOOR_SQUARED, scalar2=None, op0=ALU.max
-            )
+            for w in range(2):
+                nc.scalar.activation(
+                    out=length_sq[:, w : w + 1], in_=parts[:, w, 0:1], func=ACT.Identity, bias=parts[:, w, 1:2]
+                )
             tiles["length_sq", b] = length_sq
 
+        def length_floor(b):
+            length_sq = tiles["length_sq", b]
+            nc.scalar.activation(out=length_sq[:], in_=length_sq[:], func=ACT.Relu, bias=floor_minus[:])
+
         def length_ln(b):
-            ln_length = small.tile([P, 2], F32, name="ln_length")
-            nc.scalar.activation(out=ln_length[:], in_=tiles["length_sq", b][:], func=ACT.Ln)
-            tiles["ln_length", b] = ln_length
+            length_sq = tiles["length_sq", b]
+            nc.scalar.activation(out=length_sq[:], in_=length_sq[:], func=ACT.Ln, bias=floor_plus[:])
 
         def length_exp(b):
-            a = tiles["length_sq", b]
-            y = small.tile([P, 2], F32, name="y")
-            nc.scalar.activation(out=y[:], in_=tiles["ln_length", b][:], func=ACT.Exp, scale=-0.5)
-            step = small.tile([P, 2], F32, name="step")
-            nc.gpsimd.tensor_tensor(out=step[:], in0=a[:], in1=y[:], op=ALU.mult)
-            nc.gpsimd.tensor_tensor(out=step[:], in0=step[:], in1=y[:], op=ALU.mult)
-            nc.gpsimd.tensor_scalar(
-                out=step[:], in0=step[:], scalar1=-0.5, scalar2=1.5, op0=ALU.mult, op1=ALU.add
-            )
             inverse = small.tile([P, 2], F32, name="inverse")
-            nc.gpsimd.tensor_tensor(out=inverse[:], in0=y[:], in1=step[:], op=ALU.mult)
+            nc.scalar.activation(out=inverse[:], in_=tiles["length_sq", b][:], func=ACT.Exp, scale=-0.5)
             tiles["inverse", b] = inverse
 
         def spread_inverse(b):
             repeated = small.tile([P, 2, P], F32, name="repeated", bufs=2)
-            spread = psum_s.tile([P, PLANE], F32, name="spread")
+            spread = psum_s.tile([P, TOKENS], F32, name="spread")
             for w in range(2):
                 nc.scalar.activation(
                     out=repeated[:, w, :], in_=ones[:], func=ACT.Copy, scale=tiles["inverse", b][:, w : w + 1]
                 )
-                nc.tensor.transpose(spread[:, SECOND[w] : SECOND[w] + P], repeated[:, w, :], ident_f32[:])
+                nc.tensor.transpose(
+                    spread[:, WINDOW_START[w] : WINDOW_START[w] + P], repeated[:, w, :], ident_f32[:]
+                )
             tiles["spread", b] = spread
 
         def normalise(b):
             r = tiles["total", b]
             grouped = g_ring[b % G_RING]
-            spread = tiles["spread", b][:].rearrange("p (i j) -> p i j", j=PITCH)[:, :, 0:GRID]
             for g in range(PASSES):
                 nc.vector.tensor_tensor(
-                    out=grouped[:, g, 0:TOKENS, :].rearrange("p (i j) t -> p i j t", j=GRID),
-                    in0=r[:, PACK * g : PACK * (g + 1), :].rearrange("p t (i j) -> p i j t", j=PITCH)[
-                        :, :, 0:GRID, :
-                    ],
-                    in1=spread.unsqueeze(3).to_broadcast([P, GRID, GRID, PACK]),
+                    out=grouped[:, g, 0:TOKENS, :],
+                    in0=r[:, PACK * g : PACK * (g + 1), :].rearrange("p t n -> p n t"),
+                    in1=tiles["spread", b][:].unsqueeze(2).to_broadcast([P, TOKENS, PACK]),
                     op=ALU.mult,
                 )
 
@@ -420,25 +444,29 @@ def tile_tokenmudule_pa_t_kernel(tc, patch_tokens, fc1_w, fc1_b, out):
         with tc.manual_schedule():
             load(0)
             load(1)
-            LAST_STAGE = 7
+            LAST_STAGE = 6
             for i in range(IMAGES + LAST_STAGE):
-                when_valid(normalise, i - 6)
-                when_valid(finish, i - 7)
-                when_valid(project, i - 6)
+                when_valid(normalise, i - 5)
+                when_valid(finish, i - 6)
+                when_valid(project, i - 5)
                 when_valid(load, i + 2)
-                when_valid(token_norms, i - 5)
-                when_valid(scaled_norms, i - 2)
-                when_valid(root_ln, i - 4)
+                when_valid(mean_square, i - 1)
+                when_valid(token_norms, i - 4)
                 when_valid(weights_ln, i - 2)
-                when_valid(length_ln, i - 5)
-                when_valid(root_exp, i - 4)
+                when_valid(length_floor, i - 4)
+                when_valid(root_ln, i - 3)
+                when_valid(length_ln, i - 4)
                 when_valid(weights_exp, i - 2)
-                when_valid(length_exp, i - 5)
-                when_valid(pool_terms, i - 3)
+                when_valid(length_exp, i - 4)
                 when_valid(centre_term, i - 2)
-                when_valid(transpose_in, i)
-                when_valid(spread_inverse, i - 5)
+                when_valid(root_exp, i - 3)
+                when_valid(spread_inverse, i - 4)
                 when_valid(window_norms, i - 1)
-                when_valid(row_scale, i)
-                when_valid(residual, i - 4)
-                when_valid(cubes, i)
+                when_valid(row_scale, i - 1)
+                when_valid(weights, i - 2)
+                when_valid(pool_terms, i - 2)
+                when_valid(transpose_in, i)
+                when_valid(scaled_norms_first, i - 1)
+                when_valid(residual, i - 3)
+                when_valid(scaled_norms_second, i - 1)
+                when_valid(cubes, i - 1)

@@ -48,7 +48,7 @@ def tile_tokenmudule_pa_t_kernel(tc, patch_tokens, fc1_w, fc1_b, out):
         rows = ctx.enter_context(tc.tile_pool(name="rows", bufs=1))
         small = ctx.enter_context(tc.tile_pool(name="small", bufs=3))
         psum_x = ctx.enter_context(tc.psum_pool(name="psum_x", bufs=2))
-        psum_r = ctx.enter_context(tc.psum_pool(name="psum_r", bufs=4))
+        psum_r = ctx.enter_context(tc.psum_pool(name="psum_r", bufs=2))
         psum_s = ctx.enter_context(tc.psum_pool(name="psum_s", bufs=1))
         psum_m = ctx.enter_context(tc.psum_pool(name="psum_m", bufs=1))
 
@@ -327,32 +327,35 @@ def tile_tokenmudule_pa_t_kernel(tc, patch_tokens, fc1_w, fc1_b, out):
             nc.vector.tensor_tensor(
                 out=grid, in0=grid, in1=lines_of_rows(x_ring[b % X_RING], 0, GRID, 0), op=ALU.add
             )
-            half = BLOCKS // 2
+
+        def fold_channels(b):
+            r_sq = rows.tile([P, BLOCKS, TOKENS], F32, name="r_sq")
+            nc.scalar.activation(
+                out=r_sq[:].rearrange("p k e -> p (k e)"),
+                in_=tiles["total", b][:].rearrange("p k e -> p (k e)"),
+                func=ACT.Square,
+            )
+            folded = psum_r.tile([P, 2, P], F32, name="folded")
             for w in range(2):
-                for h in range(2):
-                    r_t = psum_r.tile([P, half, P], F32, name="r_t")
-                    for kk in range(half):
-                        nc.tensor.transpose(
-                            r_t[:, kk, :],
-                            r[:, half * h + kk, WINDOW_START[w] : WINDOW_START[w] + P],
-                            ident_f32[:],
-                        )
-                    tiles["r_t", b, w, h] = r_t
+                for k in range(BLOCKS):
+                    nc.tensor.matmul(
+                        out=folded[:, w, :],
+                        lhsT=r_sq[:, k, WINDOW_START[w] : WINDOW_START[w] + P],
+                        rhs=ident_f32[:],
+                        is_transpose=True,
+                        start=(k == 0),
+                        stop=(k == BLOCKS - 1),
+                    )
+            tiles["folded", b] = folded
 
         def token_norms(b):
-            parts = small.tile([P, 2, 2], F32, name="parts")
-            for w in range(2):
-                for h in range(2):
-                    nc.scalar.activation(
-                        out=junk_bank[:, 2 * w + h, :],
-                        in_=tiles["r_t", b, w, h][:].rearrange("p k c -> p (k c)"),
-                        func=ACT.Square,
-                        accum_out=parts[:, w, h : h + 1],
-                    )
             length_sq = small.tile([P, 2], F32, name="length_sq")
             for w in range(2):
                 nc.scalar.activation(
-                    out=length_sq[:, w : w + 1], in_=parts[:, w, 0:1], func=ACT.Identity, bias=parts[:, w, 1:2]
+                    out=junk_bank[:, w, 0:P],
+                    in_=tiles["folded", b][:, w, :],
+                    func=ACT.Identity,
+                    accum_out=length_sq[:, w : w + 1],
                 )
             tiles["length_sq", b] = length_sq
 
@@ -468,5 +471,6 @@ def tile_tokenmudule_pa_t_kernel(tc, patch_tokens, fc1_w, fc1_b, out):
                 when_valid(transpose_in, i)
                 when_valid(scaled_norms_first, i - 1)
                 when_valid(residual, i - 3)
+                when_valid(fold_channels, i - 3)
                 when_valid(scaled_norms_second, i - 1)
                 when_valid(cubes, i - 1)

@@ -18,14 +18,18 @@ TOKENS = GRID * GRID
 CHANNELS = 1024
 FEATURES = 128
 BLOCKS = CHANNELS // P
+HALF = BLOCKS // 2
+BANK = HALF * P
 PACK = 4
 PASSES = CHANNELS // (P * PACK)
 
 PITCH = GRID + 1
 LEAD = 2 * PITCH + 1
-ROW = LEAD + (GRID + 1) * PITCH
+PLANE = GRID * PITCH
+ROW = LEAD + PLANE + PITCH
 
 OFFSETS = [(di, dj) for di in (-2, -1) for dj in (-1, 0, 1)] + [(0, -1)]
+LEFT = len(OFFSETS) - 1
 CENTRE = len(OFFSETS)
 WINDOW = 9
 
@@ -34,8 +38,7 @@ FLOOR_SQUARED = 1e-24
 LN_SMALLEST = 1e-18
 
 WINDOW_START = (0, TOKENS - P)
-TOKEN_PAD = 2 * P
-STORE_GROUP = 8
+STORE_GROUP = 4
 
 FLOPS = 2 * IMAGES * TOKENS * CHANNELS * FEATURES
 
@@ -45,19 +48,17 @@ def tile_tokenmudule_pa_t_kernel(tc, patch_tokens, fc1_w, fc1_b, out):
     with ExitStack() as ctx:
         const = ctx.enter_context(tc.tile_pool(name="const", bufs=1))
         loads = ctx.enter_context(tc.tile_pool(name="loads", bufs=3))
-        rows = ctx.enter_context(tc.tile_pool(name="rows", bufs=1))
-        small = ctx.enter_context(tc.tile_pool(name="small", bufs=3))
-        psum_x = ctx.enter_context(tc.psum_pool(name="psum_x", bufs=2))
-        psum_r = ctx.enter_context(tc.psum_pool(name="psum_r", bufs=2))
-        psum_s = ctx.enter_context(tc.psum_pool(name="psum_s", bufs=1))
+        rows = ctx.enter_context(tc.tile_pool(name="rows", bufs=2))
+        small = ctx.enter_context(tc.tile_pool(name="small", bufs=4))
+        psum_x = ctx.enter_context(tc.psum_pool(name="psum_x", bufs=1))
+        psum_t = ctx.enter_context(tc.psum_pool(name="psum_t", bufs=4))
+        psum_c = ctx.enter_context(tc.psum_pool(name="psum_c", bufs=2))
         psum_m = ctx.enter_context(tc.psum_pool(name="psum_m", bufs=1))
 
         ident_bf = const.tile([P, P], BF16, name="ident_bf")
         make_identity(nc, ident_bf[:])
         ident_f32 = const.tile([P, P], F32, name="ident_f32")
         make_identity(nc, ident_f32[:])
-        ones = const.tile([P, P], F32, name="ones")
-        nc.vector.memset(ones[:], 1.0)
         ln_smallest = const.tile([P, 1], F32, name="ln_smallest")
         nc.vector.memset(ln_smallest[:], LN_SMALLEST)
         floor_plus = const.tile([P, 1], F32, name="floor_plus")
@@ -85,20 +86,25 @@ def tile_tokenmudule_pa_t_kernel(tc, patch_tokens, fc1_w, fc1_b, out):
             in_=w_grouped[:].rearrange("p g n t -> p (g n t)"),
         )
 
-        X_RING = 4
+        X_RING = 2
         x_ring = [const.tile([P, BLOCKS, ROW], BF16, name="x_pad%d" % n) for n in range(X_RING)]
         for x_pad in x_ring:
             nc.vector.memset(x_pad[:], 0.0)
-        G_RING = 2
-        g_ring = [
-            const.tile([P, PASSES, TOKEN_PAD, PACK], BF16, name="grouped%d" % n, align_bytes=64)
-            for n in range(G_RING)
+        CUBE_RING = 2
+        cube_ring = [const.tile([P, BLOCKS, ROW], F32, name="cube%d" % n) for n in range(CUBE_RING)]
+        for cube in cube_ring:
+            nc.vector.memset(cube[:], 0.0)
+        term = [
+            const.tile([P, BLOCKS, TOKENS + (GRID if o == LEFT else 0)], F32, name="term%d" % o)
+            for o in range(len(OFFSETS))
         ]
-        for grouped in g_ring:
-            nc.vector.memset(grouped[:], 0.0)
+        for o, (di, dj) in enumerate(OFFSETS):
+            if di < 0:
+                nc.vector.memset(term[o][:, :, 0 : -di * GRID], EPS_CUBED)
+        term_centre = const.tile([P, BLOCKS, TOKENS], F32, name="term_centre")
         JUNK = 4
-        junk_row = const.tile([P, JUNK, ROW], BF16, name="junk_row")
-        junk_bank = const.tile([P, JUNK, 512], BF16, name="junk_bank")
+        junk_row = const.tile([P, JUNK, PLANE], BF16, name="junk_row")
+        junk_wide = const.tile([P, 2, CHANNELS], BF16, name="junk_wide")
 
         tiles = {}
 
@@ -112,44 +118,52 @@ def tile_tokenmudule_pa_t_kernel(tc, patch_tokens, fc1_w, fc1_b, out):
             view = padded[:, k, start : start + PITCH * n_lines]
             return view.rearrange("p (i j) -> p i j", j=PITCH)[:, :, 0:GRID]
 
-        def load(b):
-            x_in = loads.tile([P, 2, CHANNELS], BF16, name="x_in")
+        def load_windows(x_tile, b):
             for w in range(2):
                 nc.sync.dma_start(
-                    out=x_in[:, w, :], in_=patch_tokens[b, WINDOW_START[w] : WINDOW_START[w] + P, :]
+                    out=x_tile[:, w, :], in_=patch_tokens[b, WINDOW_START[w] : WINDOW_START[w] + P, :]
                 )
-            tiles["x_in", b] = x_in
+
+        def load(b):
+            tiles["x_in", b] = loads.tile([P, 2, CHANNELS], BF16, name="x_in")
+            load_windows(tiles["x_in", b], b)
+
+        def load_again(b):
+            tiles["x_again", b] = loads.tile([P, 2, CHANNELS], BF16, name="x_again", bufs=2)
+            load_windows(tiles["x_again", b], b)
 
         def transpose_in(b):
             x_in = tiles["x_in", b]
             x_pad = x_ring[b % X_RING]
-            half = BLOCKS // 2
+            square = rows.tile([P, BLOCKS, PLANE], F32, name="square")
+            sum_sq = small.tile([P, BLOCKS], F32, name="sum_sq")
+            norm_sq = small.tile([P, BLOCKS, CENTRE + 1], F32, name="norm_sq")
             for h in range(2):
-                x_t = psum_x.tile([P, half, TOKENS], BF16, name="x_t")
-                for kk in range(half):
-                    cols = slice((half * h + kk) * P, (half * h + kk + 1) * P)
+                x_t = psum_x.tile([P, HALF, TOKENS], BF16, name="x_t")
+                for kk in range(HALF):
+                    cols = slice((HALF * h + kk) * P, (HALF * h + kk + 1) * P)
                     for w in range(2):
                         nc.tensor.transpose(
                             x_t[:, kk, WINDOW_START[w] : WINDOW_START[w] + P], x_in[:, w, cols], ident_bf[:]
                         )
                 nc.scalar.copy(
-                    out=lines_of_rows(x_pad[:, half * h : half * (h + 1), :], 0, GRID, 0),
+                    out=lines_of_rows(x_pad[:, HALF * h : HALF * (h + 1), :], 0, GRID, 0),
                     in_=x_t[:].rearrange("p k (i j) -> p k i j", j=GRID),
                 )
-            square = rows.tile([P, BLOCKS, ROW], F32, name="square", bufs=2)
-            sum_sq = small.tile([P, BLOCKS], F32, name="sum_sq")
-            norm_sq = small.tile([P, BLOCKS, CENTRE + 1], F32, name="norm_sq")
-            for k in range(BLOCKS):
-                nc.scalar.activation(
-                    out=square[:, k, :], in_=x_pad[:, k, :], func=ACT.Square, accum_out=sum_sq[:, k : k + 1]
-                )
-            for k in range(BLOCKS):
-                nc.scalar.activation(
-                    out=junk_row[:, k % JUNK, :],
-                    in_=square[:, k, :],
-                    func=ACT.Square,
-                    accum_out=norm_sq[:, k, CENTRE : CENTRE + 1],
-                )
+                for k in range(HALF * h, HALF * (h + 1)):
+                    nc.scalar.activation(
+                        out=square[:, k, :],
+                        in_=x_pad[:, k, LEAD : LEAD + PLANE],
+                        func=ACT.Square,
+                        accum_out=sum_sq[:, k : k + 1],
+                    )
+                for k in range(HALF * h, HALF * (h + 1)):
+                    nc.scalar.activation(
+                        out=junk_row[:, k % JUNK, :],
+                        in_=square[:, k, :],
+                        func=ACT.Square,
+                        accum_out=norm_sq[:, k, CENTRE : CENTRE + 1],
+                    )
             tiles["square", b] = square
             tiles["sum_sq", b] = sum_sq
             tiles["norm_sq", b] = norm_sq
@@ -176,17 +190,16 @@ def tile_tokenmudule_pa_t_kernel(tc, patch_tokens, fc1_w, fc1_b, out):
 
         def cubes(b):
             x_pad = x_ring[b % X_RING]
-            cube = rows.tile([P, BLOCKS, ROW], F32, name="cube", bufs=2)
+            cube = cube_ring[b % CUBE_RING]
             for k in range(BLOCKS):
                 nc.vector.scalar_tensor_tensor(
-                    out=cube[:, k, :],
-                    in0=x_pad[:, k, :],
+                    out=cube[:, k, LEAD : LEAD + PLANE],
+                    in0=x_pad[:, k, LEAD : LEAD + PLANE],
                     scalar=tiles["c", b][:, k : k + 1],
                     in1=tiles["square", b][:, k, :],
                     op0=ALU.mult,
                     op1=ALU.mult,
                 )
-            tiles["cube", b] = cube
 
         def window_norms(b):
             x_pad = x_ring[b % X_RING]
@@ -194,7 +207,7 @@ def tile_tokenmudule_pa_t_kernel(tc, patch_tokens, fc1_w, fc1_b, out):
             for o, (di, dj) in enumerate(OFFSETS):
                 n_lines = GRID + di
                 length = GRID * n_lines
-                z = rows.tile([P, BLOCKS, TOKENS], F32, name="z", bufs=len(OFFSETS))
+                z = rows.tile([P, BLOCKS, TOKENS], F32, name="z", bufs=4)
                 nc.vector.tensor_tensor(
                     out=z[:, :, 0:length].rearrange("p k (i j) -> p k i j", j=GRID),
                     in0=lines_of_rows(x_pad, -di, n_lines, 0),
@@ -243,118 +256,108 @@ def tile_tokenmudule_pa_t_kernel(tc, patch_tokens, fc1_w, fc1_b, out):
             nc.vector.tensor_tensor(out=weight[:], in0=tiles["power", b][:], in1=c_for_offsets(b), op=ALU.mult)
             tiles["weight", b] = weight
 
-        def centre_term(b):
-            centre = rows.tile([P, BLOCKS, TOKENS], F32, name="centre")
+        def centre_square(b):
+            centre = rows.tile([P, BLOCKS, TOKENS], F32, name="centre", bufs=1)
             for k in range(BLOCKS):
                 nc.scalar.activation(
                     out=centre[:, k, :].rearrange("p (i j) -> p i j", j=GRID),
-                    in_=lines_of_row(tiles["cube", b], k, 0, GRID, 0),
+                    in_=lines_of_row(cube_ring[b % CUBE_RING], k, 0, GRID, 0),
                     func=ACT.Square,
                     scale=tiles["centre_scale", b][:, k : k + 1],
                 )
             tiles["centre", b] = centre
 
-        def pool_terms(b):
-            cube = tiles["cube", b]
-            weight = tiles["weight", b]
-            total = rows.tile([P, BLOCKS, TOKENS], F32, name="total", bufs=3)
-            tiles["total", b] = total
-
-            def products(o):
-                di, dj = OFFSETS[o]
-                n_lines = GRID + di if di < 0 else GRID + 1
-                u_cubed = rows.tile([P, BLOCKS, (GRID + 1) * GRID], F32, name="u_cubed", bufs=3)
-                for k in range(BLOCKS):
-                    nc.vector.scalar_tensor_tensor(
-                        out=u_cubed[:, k, 0 : GRID * n_lines].rearrange("p (i j) -> p i j", j=GRID),
-                        in0=lines_of_row(cube, k, -di, n_lines, PITCH * di + dj),
-                        scalar=weight[:, k, o : o + 1],
-                        in1=lines_of_row(cube, k, -di, n_lines, 0),
-                        op0=ALU.mult,
-                        op1=ALU.mult,
-                    )
-                return u_cubed
-
-            def add_terms(term_ap, total_ap):
-                nc.vector.scalar_tensor_tensor(
-                    out=total_ap, in0=term_ap, scalar=EPS_CUBED, in1=total_ap, op0=ALU.max, op1=ALU.add
-                )
-
-            def add_offset(o, u_cubed):
-                di, dj = OFFSETS[o]
-                length = GRID * (GRID + di)
-                add_terms(u_cubed[:, :, 0:length], total[:, :, TOKENS - length : TOKENS])
-                if di == 0:
-                    add_terms(u_cubed[:, :, 1 : TOKENS + 1], total[:, :, :])
-
-            waiting = products(0)
+        def centre_term(b):
             for k in range(BLOCKS):
                 nc.vector.tensor_scalar(
-                    out=total[:, k, :],
+                    out=term_centre[:, k, :],
                     in0=tiles["centre", b][:, k, :],
                     scalar1=tiles["c", b][:, k : k + 1],
                     scalar2=EPS_CUBED,
                     op0=ALU.mult,
                     op1=ALU.max,
                 )
-            for o in range(1, len(OFFSETS)):
-                u_cubed = products(o)
-                if o == 1:
-                    for line in range(2):
-                        missing = 3 * (2 - line)
-                        nc.vector.tensor_scalar(
-                            out=total[:, :, GRID * line : GRID * (line + 1)],
-                            in0=total[:, :, GRID * line : GRID * (line + 1)],
-                            scalar1=missing * EPS_CUBED,
-                            scalar2=None,
-                            op0=ALU.add,
+
+        def shifted_terms(b, h):
+            cube = cube_ring[b % CUBE_RING]
+            weight = tiles["weight", b]
+
+            def lines_written(o):
+                di, dj = OFFSETS[o]
+                return GRID + 1 if o == LEFT else GRID + di
+
+            def products(o):
+                di, dj = OFFSETS[o]
+                n_lines = lines_written(o)
+                for k in range(HALF * h, HALF * (h + 1)):
+                    nc.vector.scalar_tensor_tensor(
+                        out=term[o][:, k, -di * GRID : (n_lines - di) * GRID].rearrange("p (i j) -> p i j", j=GRID),
+                        in0=lines_of_row(cube, k, -di, n_lines, PITCH * di + dj),
+                        scalar=weight[:, k, o : o + 1],
+                        in1=lines_of_row(cube, k, -di, n_lines, 0),
+                        op0=ALU.mult,
+                        op1=ALU.mult,
+                    )
+
+            def floor_at_eps(o):
+                di, dj = OFFSETS[o]
+                written = term[o][:, HALF * h : HALF * (h + 1), -di * GRID : (lines_written(o) - di) * GRID]
+                nc.vector.tensor_scalar(
+                    out=written, in0=written, scalar1=EPS_CUBED, scalar2=None, op0=ALU.max
+                )
+
+            for o in range(len(OFFSETS)):
+                products(o)
+                if o > 0:
+                    floor_at_eps(o - 1)
+            floor_at_eps(len(OFFSETS) - 1)
+
+            for w in range(2):
+                first = WINDOW_START[w]
+                total_t = psum_t.tile([P, HALF, P], F32, name="total_t")
+                for kk in range(HALF):
+                    k = HALF * h + kk
+                    nine = [term[o][:, k, first : first + P] for o in range(len(OFFSETS))]
+                    nine.append(term[LEFT][:, k, first + 1 : first + 1 + P])
+                    nine.append(term_centre[:, k, first : first + P])
+                    for n, one in enumerate(nine):
+                        nc.tensor.matmul(
+                            out=total_t[:, kk, :],
+                            lhsT=one,
+                            rhs=ident_f32[:],
+                            is_transpose=True,
+                            start=(n == 0),
+                            stop=(n == WINDOW - 1),
                         )
-                add_offset(o - 1, waiting)
-                waiting = u_cubed
-            add_offset(len(OFFSETS) - 1, waiting)
+                tiles["total_t", b, w, h] = total_t
 
         def root_ln(b):
-            flat = tiles["total", b][:].rearrange("p k e -> p (k e)")
-            nc.scalar.activation(out=flat, in_=flat, func=ACT.Ln, scale=1.0 / WINDOW)
+            r_t = rows.tile([P, 2, CHANNELS], F32, name="r_t", bufs=3)
+            for w in range(2):
+                for h in range(2):
+                    nc.scalar.activation(
+                        out=r_t[:, w, BANK * h : BANK * (h + 1)],
+                        in_=tiles["total_t", b, w, h][:].rearrange("p k c -> p (k c)"),
+                        func=ACT.Ln,
+                        scale=1.0 / WINDOW,
+                    )
+            tiles["r_t", b] = r_t
 
         def root_exp(b):
-            flat = tiles["total", b][:].rearrange("p k e -> p (k e)")
+            flat = tiles["r_t", b][:].rearrange("p w c -> p (w c)")
             nc.scalar.activation(out=flat, in_=flat, func=ACT.Exp, scale=1.0 / 3.0)
 
         def residual(b):
-            r = tiles["total", b]
-            grid = r[:].rearrange("p k (i j) -> p k i j", j=GRID)
-            nc.vector.tensor_tensor(
-                out=grid, in0=grid, in1=lines_of_rows(x_ring[b % X_RING], 0, GRID, 0), op=ALU.add
-            )
-
-        def fold_channels(b):
-            r_sq = rows.tile([P, BLOCKS, TOKENS], F32, name="r_sq")
-            nc.scalar.activation(
-                out=r_sq[:].rearrange("p k e -> p (k e)"),
-                in_=tiles["total", b][:].rearrange("p k e -> p (k e)"),
-                func=ACT.Square,
-            )
-            folded = psum_r.tile([P, 2, P], F32, name="folded")
-            for w in range(2):
-                for k in range(BLOCKS):
-                    nc.tensor.matmul(
-                        out=folded[:, w, :],
-                        lhsT=r_sq[:, k, WINDOW_START[w] : WINDOW_START[w] + P],
-                        rhs=ident_f32[:],
-                        is_transpose=True,
-                        start=(k == 0),
-                        stop=(k == BLOCKS - 1),
-                    )
-            tiles["folded", b] = folded
+            r_t = tiles["r_t", b]
+            nc.vector.tensor_tensor(out=r_t[:], in0=r_t[:], in1=tiles["x_again", b][:], op=ALU.add)
 
         def token_norms(b):
             length_sq = small.tile([P, 2], F32, name="length_sq")
             for w in range(2):
                 nc.scalar.activation(
-                    out=junk_bank[:, w, 0:P],
-                    in_=tiles["folded", b][:, w, :],
-                    func=ACT.Identity,
+                    out=junk_wide[:, w, :],
+                    in_=tiles["r_t", b][:, w, :],
+                    func=ACT.Square,
                     accum_out=length_sq[:, w : w + 1],
                 )
             tiles["length_sq", b] = length_sq
@@ -372,43 +375,45 @@ def tile_tokenmudule_pa_t_kernel(tc, patch_tokens, fc1_w, fc1_b, out):
             nc.scalar.activation(out=inverse[:], in_=tiles["length_sq", b][:], func=ACT.Exp, scale=-0.5)
             tiles["inverse", b] = inverse
 
-        def spread_inverse(b):
-            repeated = small.tile([P, 2, P], F32, name="repeated", bufs=2)
-            spread = psum_s.tile([P, TOKENS], F32, name="spread")
-            for w in range(2):
-                nc.scalar.activation(
-                    out=repeated[:, w, :], in_=ones[:], func=ACT.Copy, scale=tiles["inverse", b][:, w : w + 1]
-                )
-                nc.tensor.transpose(
-                    spread[:, WINDOW_START[w] : WINDOW_START[w] + P], repeated[:, w, :], ident_f32[:]
-                )
-            tiles["spread", b] = spread
-
         def normalise(b):
-            r = tiles["total", b]
-            grouped = g_ring[b % G_RING]
-            for g in range(PASSES):
-                nc.vector.tensor_tensor(
-                    out=grouped[:, g, 0:TOKENS, :],
-                    in0=r[:, PACK * g : PACK * (g + 1), :].rearrange("p t n -> p n t"),
-                    in1=tiles["spread", b][:].unsqueeze(2).to_broadcast([P, TOKENS, PACK]),
-                    op=ALU.mult,
+            tok_t = rows.tile([P, 2, CHANNELS], BF16, name="tok_t")
+            for w in range(2):
+                nc.vector.tensor_scalar(
+                    out=tok_t[:, w, :],
+                    in0=tiles["r_t", b][:, w, :],
+                    scalar1=tiles["inverse", b][:, w : w + 1],
+                    scalar2=None,
+                    op0=ALU.mult,
                 )
+            for g in range(PASSES):
+                tok_c = psum_c.tile([P, PACK, 2 * P], BF16, name="tok_c")
+                for t in range(PACK):
+                    cols = slice((PACK * g + t) * P, (PACK * g + t + 1) * P)
+                    for w in range(2):
+                        nc.tensor.transpose(tok_c[:, t, w * P : (w + 1) * P], tok_t[:, w, cols], ident_bf[:])
+                tiles["tok_c", b, g] = tok_c
+
+        def regroup(b):
+            grouped = rows.tile([P, PASSES, 2 * P, PACK], BF16, name="grouped", align_bytes=64)
+            nc.vector.tensor_copy(out=grouped[:, 0, :, :], in_=tiles["tok_c", b, 0][:].rearrange("p t n -> p n t"))
+            nc.scalar.copy(out=grouped[:, 1, :, :], in_=tiles["tok_c", b, 1][:].rearrange("p t n -> p n t"))
+            tiles["grouped", b] = grouped
 
         def project(b):
-            grouped = g_ring[b % G_RING]
-            codes = small.tile([P, PASSES * TOKEN_PAD], U32, name="codes", bufs=2, align_bytes=64)
-            scales = small.tile([P, PASSES * TOKEN_PAD], U8, name="scales", bufs=2, align_bytes=64)
+            codes = small.tile([P, PASSES * 2 * P], U32, name="codes", bufs=2, align_bytes=64)
+            scales = small.tile([P, PASSES * 2 * P], U8, name="scales", bufs=2, align_bytes=64)
             nc.vector.quantize_mx(
-                out=codes[:].bitcast(FP8X4), scales=scales[:], in_=grouped[:].rearrange("p g n t -> p (g n t)")
+                out=codes[:].bitcast(FP8X4),
+                scales=scales[:],
+                in_=tiles["grouped", b][:].rearrange("p g n t -> p (g n t)"),
             )
             product = psum_m.tile([P, 2, FEATURES], F32, name="product")
-            for m in range(2):
+            for w in range(2):
                 for g in range(PASSES):
-                    token_cols = slice(g * TOKEN_PAD + m * P, g * TOKEN_PAD + (m + 1) * P)
+                    token_cols = slice((2 * g + w) * P, (2 * g + w + 1) * P)
                     w_cols = slice(g * FEATURES, (g + 1) * FEATURES)
                     nc.tensor.matmul_mx(
-                        out=product[:, m, :],
+                        out=product[:, w, :],
                         lhsT=codes[:, token_cols].bitcast(FP8X4),
                         lhsT_scale=scales[:, token_cols],
                         rhs=w_codes[:, w_cols].bitcast(FP8X4),
@@ -421,7 +426,7 @@ def tile_tokenmudule_pa_t_kernel(tc, patch_tokens, fc1_w, fc1_b, out):
         def finish(b):
             n = b % STORE_GROUP
             if n == 0:
-                tiles["result"] = rows.tile([P, STORE_GROUP, 2, FEATURES], F32, name="result", bufs=2)
+                tiles["result"] = rows.tile([P, STORE_GROUP, 2, FEATURES], F32, name="result")
             result = tiles["result"]
             nc.vector.tensor_tensor(
                 out=result[:, n, :, :],
@@ -430,47 +435,49 @@ def tile_tokenmudule_pa_t_kernel(tc, patch_tokens, fc1_w, fc1_b, out):
                 op=ALU.add,
             )
             if n == STORE_GROUP - 1:
-                flat = result[:].rearrange("p n m f -> p (n m f)")
+                flat = result[:].rearrange("p n w f -> p (n w f)")
                 nc.scalar.activation(out=flat, in_=flat, func=ACT.Gelu)
                 nc.sync.dma_start(
                     out=out[b - n : b + 1, 0:P, :].rearrange("n t f -> t n f"), in_=result[:, :, 0, :]
                 )
                 nc.sync.dma_start(
                     out=out[b - n : b + 1, P:TOKENS, :].rearrange("n t f -> t n f"),
-                    in_=result[0 : TOKENS - P, :, 1, :],
+                    in_=result[P - WINDOW_START[1] : P, :, 1, :],
                 )
 
-        def when_valid(stage, b):
+        def when_valid(stage, b, *more):
             if 0 <= b < IMAGES:
-                stage(b)
+                stage(b, *more)
 
         with tc.manual_schedule():
             load(0)
             load(1)
-            LAST_STAGE = 6
+            LAST_STAGE = 8
             for i in range(IMAGES + LAST_STAGE):
-                when_valid(normalise, i - 5)
-                when_valid(finish, i - 6)
-                when_valid(project, i - 5)
+                when_valid(regroup, i - 7)
+                when_valid(finish, i - 8)
+                when_valid(centre_square, i - 3)
                 when_valid(load, i + 2)
+                when_valid(load_again, i - 4)
                 when_valid(mean_square, i - 1)
-                when_valid(token_norms, i - 4)
-                when_valid(weights_ln, i - 2)
-                when_valid(length_floor, i - 4)
-                when_valid(root_ln, i - 3)
-                when_valid(length_ln, i - 4)
-                when_valid(weights_exp, i - 2)
-                when_valid(length_exp, i - 4)
-                when_valid(centre_term, i - 2)
-                when_valid(root_exp, i - 3)
-                when_valid(spread_inverse, i - 4)
                 when_valid(window_norms, i - 1)
-                when_valid(row_scale, i - 1)
-                when_valid(weights, i - 2)
-                when_valid(pool_terms, i - 2)
                 when_valid(transpose_in, i)
+                when_valid(residual, i - 5)
+                when_valid(token_norms, i - 5)
+                when_valid(root_ln, i - 4)
+                when_valid(length_floor, i - 5)
+                when_valid(weights_ln, i - 2)
+                when_valid(length_ln, i - 5)
+                when_valid(weights_exp, i - 2)
+                when_valid(length_exp, i - 5)
+                when_valid(root_exp, i - 4)
+                when_valid(project, i - 7)
+                when_valid(row_scale, i - 1)
+                when_valid(weights, i - 3)
+                when_valid(normalise, i - 6)
+                when_valid(centre_term, i - 3)
+                when_valid(shifted_terms, i - 3, 0)
+                when_valid(shifted_terms, i - 3, 1)
                 when_valid(scaled_norms_first, i - 1)
-                when_valid(residual, i - 3)
-                when_valid(fold_channels, i - 3)
-                when_valid(scaled_norms_second, i - 1)
                 when_valid(cubes, i - 1)
+                when_valid(scaled_norms_second, i - 1)

@@ -395,8 +395,8 @@ def tile_tokenmudule_pa_t_kernel(tc, patch_tokens, fc1_w, fc1_b, out):
 
         def regroup(b):
             grouped = rows.tile([P, PASSES, 2 * P, PACK], BF16, name="grouped", align_bytes=64)
-            nc.vector.tensor_copy(out=grouped[:, 0, :, :], in_=tiles["tok_c", b, 0][:].rearrange("p t n -> p n t"))
-            nc.scalar.copy(out=grouped[:, 1, :, :], in_=tiles["tok_c", b, 1][:].rearrange("p t n -> p n t"))
+            for g in range(PASSES):
+                nc.scalar.copy(out=grouped[:, g, :, :], in_=tiles["tok_c", b, g][:].rearrange("p t n -> p n t"))
             tiles["grouped", b] = grouped
 
         def project(b):

@@ -449,35 +449,42 @@ def tile_tokenmudule_pa_t_kernel(tc, patch_tokens, fc1_w, fc1_b, out):
             if 0 <= b < IMAGES:
                 stage(b, *more)
 
+        def step(i):
+            when_valid(regroup, i - 7)
+            when_valid(finish, i - 8)
+            when_valid(centre_square, i - 3)
+            when_valid(load, i + 2)
+            when_valid(load_again, i - 4)
+            when_valid(mean_square, i - 1)
+            when_valid(window_norms, i - 1)
+            when_valid(transpose_in, i)
+            when_valid(residual, i - 5)
+            when_valid(token_norms, i - 5)
+            when_valid(root_ln, i - 4)
+            when_valid(length_floor, i - 5)
+            when_valid(weights_ln, i - 2)
+            when_valid(length_ln, i - 5)
+            when_valid(weights_exp, i - 2)
+            when_valid(length_exp, i - 5)
+            when_valid(root_exp, i - 4)
+            when_valid(project, i - 7)
+            when_valid(row_scale, i - 1)
+            when_valid(weights, i - 3)
+            when_valid(normalise, i - 6)
+            when_valid(centre_term, i - 3)
+            when_valid(shifted_terms, i - 3, 0)
+            when_valid(shifted_terms, i - 3, 1)
+            when_valid(scaled_norms_first, i - 1)
+            when_valid(cubes, i - 1)
+            when_valid(scaled_norms_second, i - 1)
+
+        LAST_STAGE = 8
+        load(0)
+        load(1)
+        for i in range(LAST_STAGE):
+            step(i)
         with tc.manual_schedule():
-            load(0)
-            load(1)
-            LAST_STAGE = 8
-            for i in range(IMAGES + LAST_STAGE):
-                when_valid(regroup, i - 7)
-                when_valid(finish, i - 8)
-                when_valid(centre_square, i - 3)
-                when_valid(load, i + 2)
-                when_valid(load_again, i - 4)
-                when_valid(mean_square, i - 1)
-                when_valid(window_norms, i - 1)
-                when_valid(transpose_in, i)
-                when_valid(residual, i - 5)
-                when_valid(token_norms, i - 5)
-                when_valid(root_ln, i - 4)
-                when_valid(length_floor, i - 5)
-                when_valid(weights_ln, i - 2)
-                when_valid(length_ln, i - 5)
-                when_valid(weights_exp, i - 2)
-                when_valid(length_exp, i - 5)
-                when_valid(root_exp, i - 4)
-                when_valid(project, i - 7)
-                when_valid(row_scale, i - 1)
-                when_valid(weights, i - 3)
-                when_valid(normalise, i - 6)
-                when_valid(centre_term, i - 3)
-                when_valid(shifted_terms, i - 3, 0)
-                when_valid(shifted_terms, i - 3, 1)
-                when_valid(scaled_norms_first, i - 1)
-                when_valid(cubes, i - 1)
-                when_valid(scaled_norms_second, i - 1)
+            for i in range(LAST_STAGE, IMAGES):
+                step(i)
+        for i in range(IMAGES, IMAGES + LAST_STAGE):
+            step(i)

from contextlib import ExitStack

import concourse.mybir as mybir
from concourse.masks import make_identity

F32 = mybir.dt.float32
BF16 = mybir.dt.bfloat16
U32 = mybir.dt.uint32
U8 = mybir.dt.uint8
FP8X4 = mybir.dt.float8_e4m3fn_x4
ACT = mybir.ActivationFunctionType
ALU = mybir.AluOpType

P = 128
IMAGES = 32
GRID = 14
TOKENS = GRID * GRID
CHANNELS = 1024
FEATURES = 128
BLOCKS = CHANNELS // P
HALF = BLOCKS // 2
BANK = HALF * P
PACK = 4
PASSES = CHANNELS // (P * PACK)

PITCH = GRID + 1
LEAD = 2 * PITCH + 1
PLANE = GRID * PITCH
ROW = LEAD + PLANE + PITCH

OFFSETS = [(di, dj) for di in (-2, -1) for dj in (-1, 0, 1)] + [(0, -1)]
LEFT = len(OFFSETS) - 1
CENTRE = len(OFFSETS)
WINDOW = 9

EPS_CUBED = 1e-18
FLOOR_SQUARED = 1e-24
LN_SMALLEST = 1e-18

WINDOW_START = (0, TOKENS - P)
STORE_GROUP = 4

FLOPS = 2 * IMAGES * TOKENS * CHANNELS * FEATURES


def tile_tokenmudule_pa_t_kernel(tc, patch_tokens, fc1_w, fc1_b, out):
    nc = tc.nc
    with ExitStack() as ctx:
        const = ctx.enter_context(tc.tile_pool(name="const", bufs=1))
        loads = ctx.enter_context(tc.tile_pool(name="loads", bufs=3))
        rows = ctx.enter_context(tc.tile_pool(name="rows", bufs=2))
        small = ctx.enter_context(tc.tile_pool(name="small", bufs=4))
        psum_x = ctx.enter_context(tc.psum_pool(name="psum_x", bufs=1))
        psum_t = ctx.enter_context(tc.psum_pool(name="psum_t", bufs=4))
        psum_c = ctx.enter_context(tc.psum_pool(name="psum_c", bufs=2))
        psum_m = ctx.enter_context(tc.psum_pool(name="psum_m", bufs=1))

        ident_bf = const.tile([P, P], BF16, name="ident_bf")
        make_identity(nc, ident_bf[:])
        ident_f32 = const.tile([P, P], F32, name="ident_f32")
        make_identity(nc, ident_f32[:])
        ln_smallest = const.tile([P, 1], F32, name="ln_smallest")
        nc.vector.memset(ln_smallest[:], LN_SMALLEST)
        floor_plus = const.tile([P, 1], F32, name="floor_plus")
        nc.vector.memset(floor_plus[:], FLOOR_SQUARED)
        floor_minus = const.tile([P, 1], F32, name="floor_minus")
        nc.vector.memset(floor_minus[:], -FLOOR_SQUARED)

        bias_bf = const.tile([P, FEATURES], BF16, name="bias_bf")
        nc.sync.dma_start(out=bias_bf[:], in_=fc1_b.partition_broadcast(P))
        bias = const.tile([P, FEATURES], F32, name="bias")
        nc.vector.tensor_copy(out=bias[:], in_=bias_bf[:])

        w_raw = const.tile([P, BLOCKS, FEATURES], BF16, name="w_raw")
        nc.sync.dma_start(out=w_raw[:], in_=fc1_w.rearrange("(a p) n -> p a n", p=P))
        w_grouped = const.tile([P, PASSES, FEATURES, PACK], BF16, name="w_grouped", align_bytes=64)
        for g in range(PASSES):
            nc.vector.tensor_copy(
                out=w_grouped[:, g, :, :], in_=w_raw[:, PACK * g : PACK * (g + 1), :].rearrange("p t n -> p n t")
            )
        w_codes = const.tile([P, PASSES * FEATURES], U32, name="w_codes", align_bytes=64)
        w_scales = const.tile([P, PASSES * FEATURES], U8, name="w_scales", align_bytes=64)
        nc.vector.quantize_mx(
            out=w_codes[:].bitcast(FP8X4),
            scales=w_scales[:],
            in_=w_grouped[:].rearrange("p g n t -> p (g n t)"),
        )

        X_RING = 2
        x_ring = [const.tile([P, BLOCKS, ROW], BF16, name="x_pad%d" % n) for n in range(X_RING)]
        for x_pad in x_ring:
            nc.vector.memset(x_pad[:], 0.0)
        CUBE_RING = 2
        cube_ring = [const.tile([P, BLOCKS, ROW], F32, name="cube%d" % n) for n in range(CUBE_RING)]
        for cube in cube_ring:
            nc.vector.memset(cube[:], 0.0)
        term = [
            const.tile([P, BLOCKS, TOKENS + (GRID if o == LEFT else 0)], F32, name="term%d" % o)
            for o in range(len(OFFSETS))
        ]
        for o, (di, dj) in enumerate(OFFSETS):
            if di < 0:
                nc.vector.memset(term[o][:, :, 0 : -di * GRID], EPS_CUBED)
        term_centre = const.tile([P, BLOCKS, TOKENS], F32, name="term_centre")
        JUNK = 4
        junk_row = const.tile([P, JUNK, PLANE], BF16, name="junk_row")
        junk_wide = const.tile([P, 2, CHANNELS], BF16, name="junk_wide")

        tiles = {}

        def lines_of_rows(padded, first_line, n_lines, shift):
            start = LEAD + PITCH * first_line + shift
            view = padded[:, :, start : start + PITCH * n_lines]
            return view.rearrange("p k (i j) -> p k i j", j=PITCH)[:, :, :, 0:GRID]

        def lines_of_row(padded, k, first_line, n_lines, shift):
            start = LEAD + PITCH * first_line + shift
            view = padded[:, k, start : start + PITCH * n_lines]
            return view.rearrange("p (i j) -> p i j", j=PITCH)[:, :, 0:GRID]

        def load_windows(x_tile, b):
            for w in range(2):
                nc.sync.dma_start(
                    out=x_tile[:, w, :], in_=patch_tokens[b, WINDOW_START[w] : WINDOW_START[w] + P, :]
                )

        def load(b):
            tiles["x_in", b] = loads.tile([P, 2, CHANNELS], BF16, name="x_in")
            load_windows(tiles["x_in", b], b)

        def load_again(b):
            tiles["x_again", b] = loads.tile([P, 2, CHANNELS], BF16, name="x_again", bufs=2)
            load_windows(tiles["x_again", b], b)

        def transpose_in(b):
            x_in = tiles["x_in", b]
            x_pad = x_ring[b % X_RING]
            square = rows.tile([P, BLOCKS, PLANE], F32, name="square")
            sum_sq = small.tile([P, BLOCKS], F32, name="sum_sq")
            norm_sq = small.tile([P, BLOCKS, CENTRE + 1], F32, name="norm_sq")
            for h in range(2):
                x_t = psum_x.tile([P, HALF, TOKENS], BF16, name="x_t")
                for kk in range(HALF):
                    cols = slice((HALF * h + kk) * P, (HALF * h + kk + 1) * P)
                    for w in range(2):
                        nc.tensor.transpose(
                            x_t[:, kk, WINDOW_START[w] : WINDOW_START[w] + P], x_in[:, w, cols], ident_bf[:]
                        )
                nc.scalar.copy(
                    out=lines_of_rows(x_pad[:, HALF * h : HALF * (h + 1), :], 0, GRID, 0),
                    in_=x_t[:].rearrange("p k (i j) -> p k i j", j=GRID),
                )
                for k in range(HALF * h, HALF * (h + 1)):
                    nc.scalar.activation(
                        out=square[:, k, :],
                        in_=x_pad[:, k, LEAD : LEAD + PLANE],
                        func=ACT.Square,
                        accum_out=sum_sq[:, k : k + 1],
                    )
                for k in range(HALF * h, HALF * (h + 1)):
                    nc.scalar.activation(
                        out=junk_row[:, k % JUNK, :],
                        in_=square[:, k, :],
                        func=ACT.Square,
                        accum_out=norm_sq[:, k, CENTRE : CENTRE + 1],
                    )
            tiles["square", b] = square
            tiles["sum_sq", b] = sum_sq
            tiles["norm_sq", b] = norm_sq

        def mean_square(b):
            mean_sq = small.tile([P, BLOCKS], F32, name="mean_sq")
            nc.vector.tensor_scalar(
                out=mean_sq[:],
                in0=tiles["sum_sq", b][:],
                scalar1=1.0 / TOKENS,
                scalar2=1e-20,
                op0=ALU.mult,
                op1=ALU.max,
            )
            tiles["mean_sq", b] = mean_sq

        def row_scale(b):
            c = small.tile([P, BLOCKS], F32, name="c")
            nc.vector.reciprocal(out=c[:], in_=tiles["mean_sq", b][:])
            tiles["c", b] = c

        def c_for_offsets(b):
            return tiles["c", b][:].unsqueeze(2).to_broadcast([P, BLOCKS, CENTRE + 1])

        def cubes(b):
            x_pad = x_ring[b % X_RING]
            cube = cube_ring[b % CUBE_RING]
            for k in range(BLOCKS):
                nc.vector.scalar_tensor_tensor(
                    out=cube[:, k, LEAD : LEAD + PLANE],
                    in0=x_pad[:, k, LEAD : LEAD + PLANE],
                    scalar=tiles["c", b][:, k : k + 1],
                    in1=tiles["square", b][:, k, :],
                    op0=ALU.mult,
                    op1=ALU.mult,
                )

        def window_norms(b):
            x_pad = x_ring[b % X_RING]
            norm_sq = tiles["norm_sq", b]
            for o, (di, dj) in enumerate(OFFSETS):
                n_lines = GRID + di
                length = GRID * n_lines
                z = rows.tile([P, BLOCKS, TOKENS], F32, name="z", bufs=4)
                nc.vector.tensor_tensor(
                    out=z[:, :, 0:length].rearrange("p k (i j) -> p k i j", j=GRID),
                    in0=lines_of_rows(x_pad, -di, n_lines, 0),
                    in1=lines_of_rows(x_pad, -di, n_lines, PITCH * di + dj),
                    op=ALU.mult,
                )
                for k in range(BLOCKS):
                    nc.scalar.activation(
                        out=z[:, k, 0:length],
                        in_=z[:, k, 0:length],
                        func=ACT.Square,
                        accum_out=norm_sq[:, k, o : o + 1],
                    )

        def scaled_norms_first(b):
            scaled = small.tile([P, BLOCKS, CENTRE + 1], F32, name="scaled")
            nc.vector.scalar_tensor_tensor(
                out=scaled[:],
                in0=tiles["norm_sq", b][:],
                scalar=FLOOR_SQUARED,
                in1=c_for_offsets(b),
                op0=ALU.max,
                op1=ALU.mult,
            )
            tiles["scaled", b] = scaled

        def scaled_norms_second(b):
            scaled = tiles["scaled", b]
            nc.vector.tensor_tensor(out=scaled[:], in0=scaled[:], in1=c_for_offsets(b), op=ALU.mult)

        def weights_ln(b):
            scaled = tiles["scaled", b]
            nc.scalar.activation(out=scaled[:], in_=scaled[:], func=ACT.Ln, bias=ln_smallest[:])

        def weights_exp(b):
            ln_scaled = tiles["scaled", b]
            power = small.tile([P, BLOCKS, CENTRE + 1], F32, name="power")
            nc.scalar.activation(out=power[:], in_=ln_scaled[:], func=ACT.Exp, scale=-1.5)
            centre_scale = small.tile([P, BLOCKS], F32, name="centre_scale")
            nc.scalar.activation(out=centre_scale[:], in_=ln_scaled[:, :, CENTRE], func=ACT.Exp, scale=-0.75)
            tiles["power", b] = power
            tiles["centre_scale", b] = centre_scale

        def weights(b):
            weight = small.tile([P, BLOCKS, CENTRE + 1], F32, name="weight")
            nc.vector.tensor_tensor(out=weight[:], in0=tiles["power", b][:], in1=c_for_offsets(b), op=ALU.mult)
            tiles["weight", b] = weight

        def centre_square(b):
            centre = rows.tile([P, BLOCKS, TOKENS], F32, name="centre", bufs=1)
            for k in range(BLOCKS):
                nc.scalar.activation(
                    out=centre[:, k, :].rearrange("p (i j) -> p i j", j=GRID),
                    in_=lines_of_row(cube_ring[b % CUBE_RING], k, 0, GRID, 0),
                    func=ACT.Square,
                    scale=tiles["centre_scale", b][:, k : k + 1],
                )
            tiles["centre", b] = centre

        def centre_term(b):
            for k in range(BLOCKS):
                nc.vector.tensor_scalar(
                    out=term_centre[:, k, :],
                    in0=tiles["centre", b][:, k, :],
                    scalar1=tiles["c", b][:, k : k + 1],
                    scalar2=EPS_CUBED,
                    op0=ALU.mult,
                    op1=ALU.max,
                )

        def shifted_terms(b, h):
            cube = cube_ring[b % CUBE_RING]
            weight = tiles["weight", b]

            def lines_written(o):
                di, dj = OFFSETS[o]
                return GRID + 1 if o == LEFT else GRID + di

            def products(o):
                di, dj = OFFSETS[o]
                n_lines = lines_written(o)
                for k in range(HALF * h, HALF * (h + 1)):
                    nc.vector.scalar_tensor_tensor(
                        out=term[o][:, k, -di * GRID : (n_lines - di) * GRID].rearrange("p (i j) -> p i j", j=GRID),
                        in0=lines_of_row(cube, k, -di, n_lines, PITCH * di + dj),
                        scalar=weight[:, k, o : o + 1],
                        in1=lines_of_row(cube, k, -di, n_lines, 0),
                        op0=ALU.mult,
                        op1=ALU.mult,
                    )

            def floor_at_eps(o):
                di, dj = OFFSETS[o]
                written = term[o][:, HALF * h : HALF * (h + 1), -di * GRID : (lines_written(o) - di) * GRID]
                nc.vector.tensor_scalar(
                    out=written, in0=written, scalar1=EPS_CUBED, scalar2=None, op0=ALU.max
                )

            for o in range(len(OFFSETS)):
                products(o)
                if o > 0:
                    floor_at_eps(o - 1)
            floor_at_eps(len(OFFSETS) - 1)

            for w in range(2):
                first = WINDOW_START[w]
                total_t = psum_t.tile([P, HALF, P], F32, name="total_t")
                for kk in range(HALF):
                    k = HALF * h + kk
                    nine = [term[o][:, k, first : first + P] for o in range(len(OFFSETS))]
                    nine.append(term[LEFT][:, k, first + 1 : first + 1 + P])
                    nine.append(term_centre[:, k, first : first + P])
                    for n, one in enumerate(nine):
                        nc.tensor.matmul(
                            out=total_t[:, kk, :],
                            lhsT=one,
                            rhs=ident_f32[:],
                            is_transpose=True,
                            start=(n == 0),
                            stop=(n == WINDOW - 1),
                        )
                tiles["total_t", b, w, h] = total_t

        def root_ln(b):
            r_t = rows.tile([P, 2, CHANNELS], F32, name="r_t", bufs=3)
            for w in range(2):
                for h in range(2):
                    nc.scalar.activation(
                        out=r_t[:, w, BANK * h : BANK * (h + 1)],
                        in_=tiles["total_t", b, w, h][:].rearrange("p k c -> p (k c)"),
                        func=ACT.Ln,
                        scale=1.0 / WINDOW,
                    )
            tiles["r_t", b] = r_t

        def root_exp(b):
            flat = tiles["r_t", b][:].rearrange("p w c -> p (w c)")
            nc.scalar.activation(out=flat, in_=flat, func=ACT.Exp, scale=1.0 / 3.0)

        def residual(b):
            r_t = tiles["r_t", b]
            nc.vector.tensor_tensor(out=r_t[:], in0=r_t[:], in1=tiles["x_again", b][:], op=ALU.add)

        def token_norms(b):
            length_sq = small.tile([P, 2], F32, name="length_sq")
            for w in range(2):
                nc.scalar.activation(
                    out=junk_wide[:, w, :],
                    in_=tiles["r_t", b][:, w, :],
                    func=ACT.Square,
                    accum_out=length_sq[:, w : w + 1],
                )
            tiles["length_sq", b] = length_sq

        def length_floor(b):
            length_sq = tiles["length_sq", b]
            nc.scalar.activation(out=length_sq[:], in_=length_sq[:], func=ACT.Relu, bias=floor_minus[:])

        def length_ln(b):
            length_sq = tiles["length_sq", b]
            nc.scalar.activation(out=length_sq[:], in_=length_sq[:], func=ACT.Ln, bias=floor_plus[:])

        def length_exp(b):
            inverse = small.tile([P, 2], F32, name="inverse")
            nc.scalar.activation(out=inverse[:], in_=tiles["length_sq", b][:], func=ACT.Exp, scale=-0.5)
            tiles["inverse", b] = inverse

        def normalise(b):
            tok_t = rows.tile([P, 2, CHANNELS], BF16, name="tok_t")
            for w in range(2):
                nc.vector.tensor_scalar(
                    out=tok_t[:, w, :],
                    in0=tiles["r_t", b][:, w, :],
                    scalar1=tiles["inverse", b][:, w : w + 1],
                    scalar2=None,
                    op0=ALU.mult,
                )
            for g in range(PASSES):
                tok_c = psum_c.tile([P, PACK, 2 * P], BF16, name="tok_c")
                for t in range(PACK):
                    cols = slice((PACK * g + t) * P, (PACK * g + t + 1) * P)
                    for w in range(2):
                        nc.tensor.transpose(tok_c[:, t, w * P : (w + 1) * P], tok_t[:, w, cols], ident_bf[:])
                tiles["tok_c", b, g] = tok_c

        def regroup(b):
            grouped = rows.tile([P, PASSES, 2 * P, PACK], BF16, name="grouped", align_bytes=64)
            for g in range(PASSES):
                nc.scalar.copy(out=grouped[:, g, :, :], in_=tiles["tok_c", b, g][:].rearrange("p t n -> p n t"))
            tiles["grouped", b] = grouped

        def project(b):
            codes = small.tile([P, PASSES * 2 * P], U32, name="codes", bufs=2, align_bytes=64)
            scales = small.tile([P, PASSES * 2 * P], U8, name="scales", bufs=2, align_bytes=64)
            nc.vector.quantize_mx(
                out=codes[:].bitcast(FP8X4),
                scales=scales[:],
                in_=tiles["grouped", b][:].rearrange("p g n t -> p (g n t)"),
            )
            product = psum_m.tile([P, 2, FEATURES], F32, name="product")
            for w in range(2):
                for g in range(PASSES):
                    token_cols = slice((2 * g + w) * P, (2 * g + w + 1) * P)
                    w_cols = slice(g * FEATURES, (g + 1) * FEATURES)
                    nc.tensor.matmul_mx(
                        out=product[:, w, :],
                        lhsT=codes[:, token_cols].bitcast(FP8X4),
                        lhsT_scale=scales[:, token_cols],
                        rhs=w_codes[:, w_cols].bitcast(FP8X4),
                        rhs_scale=w_scales[:, w_cols],
                        start=(g == 0),
                        stop=(g == PASSES - 1),
                    )
            tiles["product", b] = product

        def finish(b):
            n = b % STORE_GROUP
            if n == 0:
                tiles["result"] = rows.tile([P, STORE_GROUP, 2, FEATURES], F32, name="result")
            result = tiles["result"]
            nc.vector.tensor_tensor(
                out=result[:, n, :, :],
                in0=tiles["product", b][:],
                in1=bias[:].unsqueeze(1).to_broadcast([P, 2, FEATURES]),
                op=ALU.add,
            )
            if n == STORE_GROUP - 1:
                flat = result[:].rearrange("p n w f -> p (n w f)")
                nc.scalar.activation(out=flat, in_=flat, func=ACT.Gelu)
                nc.sync.dma_start(
                    out=out[b - n : b + 1, 0:P, :].rearrange("n t f -> t n f"), in_=result[:, :, 0, :]
                )
                nc.sync.dma_start(
                    out=out[b - n : b + 1, P:TOKENS, :].rearrange("n t f -> t n f"),
                    in_=result[P - WINDOW_START[1] : P, :, 1, :],
                )

        def when_valid(stage, b, *more):
            if 0 <= b < IMAGES:
                stage(b, *more)

        def step(i):
            when_valid(regroup, i - 7)
            when_valid(finish, i - 8)
            when_valid(centre_square, i - 3)
            when_valid(load, i + 2)
            when_valid(load_again, i - 4)
            when_valid(mean_square, i - 1)
            when_valid(window_norms, i - 1)
            when_valid(transpose_in, i)
            when_valid(residual, i - 5)
            when_valid(token_norms, i - 5)
            when_valid(root_ln, i - 4)
            when_valid(length_floor, i - 5)
            when_valid(weights_ln, i - 2)
            when_valid(length_ln, i - 5)
            when_valid(weights_exp, i - 2)
            when_valid(length_exp, i - 5)
            when_valid(root_exp, i - 4)
            when_valid(project, i - 7)
            when_valid(row_scale, i - 1)
            when_valid(weights, i - 3)
            when_valid(normalise, i - 6)
            when_valid(centre_term, i - 3)
            when_valid(shifted_terms, i - 3, 0)
            when_valid(shifted_terms, i - 3, 1)
            when_valid(scaled_norms_first, i - 1)
            when_valid(cubes, i - 1)
            when_valid(scaled_norms_second, i - 1)

        LAST_STAGE = 8
        load(0)
        load(1)
        for i in range(LAST_STAGE):
            step(i)
        with tc.manual_schedule():
            for i in range(LAST_STAGE, IMAGES):
                step(i)
        for i in range(IMAGES, IMAGES + LAST_STAGE):
            step(i)
